import numpy as np
import ml_dtypes


def mxq(x, axis, fmt="e4m3"):
    dtype, down = {"e4m3": (ml_dtypes.float8_e4m3fn, 7), "e5m2": (ml_dtypes.float8_e5m2, 14)}[fmt]
    v = np.moveaxis(np.asarray(x, np.float32).astype(ml_dtypes.bfloat16).astype(np.float64), axis, -1)
    blocks = v.reshape(v.shape[:-1] + (-1, 32))
    amax = np.abs(blocks).max(-1, keepdims=True)
    byte = np.maximum(np.where(amax > 0, np.frexp(amax)[1] - 1 + 127, 0) - down, 1)
    scale = np.exp2(byte - 127.0)
    codes = (blocks / scale).astype(np.float32).astype(dtype).astype(np.float64)
    return np.moveaxis((codes * scale).reshape(v.shape), -1, axis)


WIDE = False


def mx_kscale(k):
    if not WIDE:
        return np.ones(k)
    levels = np.array([10, -10, 5, -5, 0])
    if k % 512:
        return np.exp2(np.random.permutation(np.resize(levels, k // 32))).repeat(32)
    a = np.empty((k // 512, 16))
    for p in range(k // 512):
        a[p, :8] = np.random.permutation(np.resize(levels, 8))
        for g in range(8):
            far = levels[np.abs(levels - a[p, g]) >= 10]
            a[p, g + 8] = far[np.random.randint(len(far))]
    return np.exp2(a.ravel()).repeat(32)


BF16 = ml_dtypes.bfloat16


def bf(x):
    return np.asarray(x, np.float32).astype(BF16)


def f64(x):
    return np.asarray(x).astype(np.float64)


B, D, U1, U2 = 8192, 512, 512, 256
THRESHOLD = 1.0


def setup_inputs():
    s, t = mx_kscale(D), mx_kscale(U1)
    c = s / s.mean()
    u = np.random.random(B)
    target = np.where(np.random.random(B) < 0.5, 0.5 + 0.35 * u, 1.15 + 0.45 * u)
    g = np.random.standard_normal((B, D)) * c
    x = g * (target / np.mean(np.abs(g), axis=1))[:, None]
    return {"x": bf(x),
            "W1": bf(np.random.standard_normal((U1, D)) / np.sqrt(D) / c[None, :] * t[:, None]),
            "b1": bf(np.random.standard_normal(U1) * 0.3 * t),
            "W2": bf(np.random.standard_normal((U2, D)) / np.sqrt(D) / c[None, :] * t[:U2, None]),
            "b2": bf(np.random.standard_normal(U2) * 0.3 * t[:U2]),
            "Wf": bf(np.random.standard_normal((D, U1)) * 1.5 / np.sqrt(U1) / t[None, :]),
            "bf": bf(np.random.standard_normal(D) * 0.3)}


def reference(x, W1, b1, W2, b2, Wf, bf):
    x = f64(x)
    mask = np.mean(np.abs(x), axis=1) > THRESHOLD
    xq = mxq(x, 1, "e4m3")
    o1 = np.maximum((xq @ mxq(f64(W1), 1, "e4m3").T) + f64(b1), 0.0)
    o2 = np.maximum((xq @ mxq(f64(W2), 1, "e4m3").T) + f64(b2), 0.0)
    final_dim = W1.shape[0]
    o2p = np.pad(o2, ((0, 0), (0, final_dim - o2.shape[1])))
    branch_out = np.where(mask[:, None], o1, o2p)
    return (mxq(branch_out, 1, "e4m3") @ mxq(f64(Wf), 1, "e4m3").T) + f64(bf)

@@ -1,0 +1,239 @@
+from contextlib import ExitStack
+
+import concourse.mybir as mybir
+from concourse.masks import make_identity
+
+F32 = mybir.dt.float32
+BF16 = mybir.dt.bfloat16
+U32 = mybir.dt.uint32
+U8 = mybir.dt.uint8
+FP8X4 = mybir.dt.float8_e4m3fn_x4
+ALU = mybir.AluOpType
+ACT = mybir.ActivationFunctionType
+
+P = 128
+H = 64
+B, D, U1, U2 = 8192, 512, 512, 256
+FLOPS = 2 * B * D * (U1 + U2) + 2 * B * U1 * D
+CH = 512
+HC = CH // 2
+SL = CH + HC
+NCH = B // CH
+SUP = 1024
+NSUP = B // SUP
+
+
+def tile_dynamiclayer_t_kernel(tc, x, W1, b1, W2, b2, Wf, bf, out):
+    nc = tc.nc
+    with ExitStack() as ctx:
+        const = ctx.enter_context(tc.tile_pool(name="const", bufs=1))
+        xpool = ctx.enter_context(tc.tile_pool(name="xpool", bufs=1))
+        work = ctx.enter_context(tc.tile_pool(name="work", bufs=2))
+        opool = ctx.enter_context(tc.tile_pool(name="opool", bufs=3))
+        ps_x = ctx.enter_context(tc.psum_pool(name="ps_x", bufs=2))
+        ps_z = ctx.enter_context(tc.psum_pool(name="ps_z", bufs=3))
+        ps_y = ctx.enter_context(tc.psum_pool(name="ps_y", bufs=2))
+        ps_m = ctx.enter_context(tc.psum_pool(name="ps_m", bufs=1))
+
+        w1_sb = const.tile([P, 4 * D], BF16)
+        w2_sb = const.tile([P, 4 * D], BF16)
+        wf_sb = const.tile([P, 4 * 2 * U1], BF16)
+        nc.vector.memset(w2_sb[H:P, :], 0.0)
+        nc.sync.dma_start(out=w1_sb[:], in_=W1.rearrange("(m t) k -> m (t k)", t=4))
+        nc.sync.dma_start(out=w2_sb[0:H, :], in_=W2.rearrange("(m t) k -> m (t k)", t=4))
+        x_view = x.rearrange("(s p r) k -> s p (r k)", p=P, r=SUP // P)
+        xs = []
+        for s in range(NSUP):
+            xt_sb = xpool.tile([P, (SUP // P) * D], BF16, name="x%d" % s)
+            xs.append(xt_sb)
+        nc.sync.dma_start(out=xs[0][:], in_=x_view[0])
+        wf_dst = wf_sb[:].rearrange("p (a h u) -> p a h u", a=4, h=2)
+        for h in range(2):
+            nc.sync.dma_start(out=wf_dst[:, :, h, :], in_=Wf.rearrange("(a p) u -> p a u", p=P))
+        for s in range(1, NSUP):
+            nc.sync.dma_start(out=xs[s][:], in_=x_view[s])
+
+        bb1 = const.tile([P, 4], BF16)
+        bb1r = const.tile([P, 4], BF16)
+        bb2 = const.tile([P, 4], BF16)
+        b1v = b1.rearrange("(p t) -> p t", t=4)
+        b2v = b2.rearrange("(p t) -> p t", t=4)
+        with nc.allow_non_contiguous_dma(reason="four bias values to a partition"):
+            nc.scalar.dma_start(out=bb1[:], in_=b1v)
+            nc.scalar.dma_start(out=bb1r[0:H, :], in_=b1v[H:P, :])
+            nc.scalar.dma_start(out=bb1r[H:P, :], in_=b1v[0:H, :])
+            nc.scalar.dma_start(out=bb2[0:H, :], in_=b2v)
+            nc.scalar.dma_start(out=bb2[H:P, :], in_=b2v)
+        bfb = const.tile([P, D], BF16)
+        nc.gpsimd.dma_start(out=bfb[:], in_=bf.partition_broadcast(P))
+
+        ident_f = const.tile([P, P], F32)
+        make_identity(nc, ident_f[:])
+        ident_b = const.tile([P, P], BF16)
+        make_identity(nc, ident_b[:])
+
+        bc1 = const.tile([P, 4], F32)
+        bc1r = const.tile([P, 4], F32)
+        bc2 = const.tile([P, 4], F32)
+        nc.vector.tensor_copy(out=bc1[:], in_=bb1[:])
+        nc.vector.tensor_copy(out=bc1r[:], in_=bb1r[:])
+        nc.vector.tensor_copy(out=bc2[:], in_=bb2[:])
+
+        def bank_of_transposes(srcs, dsts, copy_engine):
+            xt = ps_x.tile([P, 512], F32, tag="xt")
+            for n in range(4):
+                nc.tensor.transpose(xt[:, n * P:(n + 1) * P], srcs[n], ident_f[:])
+            src = xt[:].rearrange("p (r u j) -> p r j u", r=2, u=2)
+            for dst in dsts:
+                if copy_engine == "s":
+                    nc.scalar.copy(out=dst, in_=src)
+                else:
+                    nc.vector.tensor_copy(out=dst, in_=src)
+
+        def halves(src_f32, tile_index):
+            base = tile_index * 256
+            return [src_f32[:, base:base + 2 * P:2], src_f32[:, base + 1:base + 2 * P:2]]
+
+        def stationary(w_sb, engine):
+            g = const.tile([P, 4 * 2 * P * 4], BF16, align_bytes=64, name="g_" + engine)
+            codes = const.tile([P, 4 * 2 * P], U32, align_bytes=64, name="c_" + engine)
+            scales = const.tile([P, 4 * 2 * P], U8, align_bytes=64, name="s_" + engine)
+            gv = g[:].bitcast(F32).rearrange("p (t d j u) -> p t d j u", t=4, d=2, u=2)
+            wv = w_sb[:].bitcast(F32)
+            for q in range(2):
+                bank_of_transposes(halves(wv, 2 * q) + halves(wv, 2 * q + 1),
+                                   [gv[:, 2 * q:2 * q + 2, 0], gv[:, 2 * q:2 * q + 2, 1]], engine)
+            nc.vector.quantize_mx(out=codes[:].bitcast(FP8X4), scales=scales[:], in_=g[:])
+            return codes, scales
+
+        w1c, w1s = stationary(w1_sb, "v")
+        w2c, w2s = stationary(w2_sb, "s")
+
+        def slot(codes, scales, t, shifted):
+            lo = t * 2 * P + (H if shifted else 0)
+            return codes[:, lo:lo + P].bitcast(FP8X4), scales[:, lo:lo + P]
+
+        wfq = []
+
+        def prepare_wf():
+            wv = wf_sb[:].bitcast(F32)
+            for shifted in range(2):
+                g = const.tile([P, D * 4], BF16, align_bytes=64, name="wfg%d" % shifted)
+                codes = const.tile([P, D], U32, align_bytes=64, name="wfc%d" % shifted)
+                scales = const.tile([P, D], U8, align_bytes=64, name="wfs%d" % shifted)
+                gv = g[:].bitcast(F32).rearrange("p (a j u) -> p a j u", a=4, u=2)
+                for q in range(2):
+                    srcs = []
+                    for a in (2 * q, 2 * q + 1):
+                        for u in range(2):
+                            lo = a * 512 + shifted * P + u
+                            srcs.append(wv[:, lo:lo + 256:2])
+                    bank_of_transposes(srcs, [gv[:, 2 * q:2 * q + 2]], "v")
+                nc.vector.quantize_mx(out=codes[:].bitcast(FP8X4), scales=scales[:], in_=g[:])
+                wfq.append((codes, scales))
+
+        state = {}
+
+        def front(c):
+            s, h = c // 2, c % 2
+            xc_sb = xs[s][:, h * 4 * D:(h + 1) * 4 * D]
+            ssum = work.tile([P, 4], F32, tag="ssum")
+            for r in range(4):
+                junk = work.tile([P, D], BF16, tag="junk")
+                nc.scalar.activation(out=junk[:], in_=xc_sb[:, r * D:(r + 1) * D], func=ACT.Abs,
+                                     accum_out=ssum[:, r:r + 1])
+            mcol = work.tile([P, 4], BF16, tag="mcol")
+            nc.gpsimd.tensor_scalar(out=mcol[:], in0=ssum[:], scalar1=float(D), scalar2=None,
+                                    op0=ALU.is_gt)
+            nl = work.tile([P, 2 * P], BF16, tag="nl")
+            nc.gpsimd.tensor_scalar(
+                out=nl[:].rearrange("p (r h c) -> p r h c", r=2, h=2),
+                in0=ssum[:].rearrange("p (h r) -> p r h", h=2).unsqueeze(3).to_broadcast([P, 2, 2, H]),
+                scalar1=float(D), scalar2=None, op0=ALU.is_le)
+            xg = work.tile([P, CH * 4], BF16, tag="xg", align_bytes=64)
+            gv = xg[:].bitcast(F32).rearrange("p (r j u) -> p r j u", r=4, u=2)
+            xv = xc_sb.bitcast(F32)
+            for q in range(2):
+                bank_of_transposes(halves(xv, 2 * q) + halves(xv, 2 * q + 1), [gv[:, 2 * q:2 * q + 2]], "s")
+            xc = work.tile([P, CH], U32, tag="xc", align_bytes=64)
+            xsc = work.tile([P, CH], U8, tag="xsc", align_bytes=64)
+            nc.vector.quantize_mx(out=xc[:].bitcast(FP8X4), scales=xsc[:], in_=xg[:])
+            state[("x", c)] = (xc, xsc, mcol, nl)
+
+        def mid(c):
+            xc, xsc, mcol, nl = state[("x", c)]
+            mb = ps_m.tile([P, CH + HC], BF16, tag="mb")
+            for r in range(4):
+                nc.tensor.matmul(out=mb[:, r * P:(r + 1) * P], lhsT=mcol[:, r:r + 1].to_broadcast([P, P]),
+                                 rhs=ident_b[:], start=True, stop=True)
+            for r in range(2):
+                nc.tensor.matmul(out=mb[:, CH + r * P:CH + (r + 1) * P], lhsT=nl[:, r * P:(r + 1) * P],
+                                 rhs=ident_b[:], start=True, stop=True)
+            half = [(xc[:, g * HC:(g + 1) * HC].bitcast(FP8X4), xsc[:, g * HC:(g + 1) * HC]) for g in range(2)]
+            rr = work.tile([P, 4 * SL], BF16, tag="rr")
+            for t in range(4):
+                z = ps_z.tile([P, CH], F32, tag="z")
+                for g in range(2):
+                    wc, ws = slot(w1c, w1s, t, g == 1)
+                    nc.tensor.matmul_mx(out=z[:, g * HC:(g + 1) * HC], lhsT=wc, lhsT_scale=ws,
+                                        rhs=half[g][0], rhs_scale=half[g][1], start=True, stop=True)
+                for g in range(2):
+                    bias = bc1r if g == 1 else bc1
+                    nc.scalar.activation(out=rr[:, t * SL + g * HC:t * SL + (g + 1) * HC],
+                                         in_=z[:, g * HC:(g + 1) * HC], func=ACT.Relu,
+                                         bias=bias[:, t:t + 1], scale=1.0)
+            for q in range(2):
+                z = ps_z.tile([P, CH], F32, tag="z")
+                for tt in range(2):
+                    t = 2 * q + tt
+                    for g in range(2):
+                        wc, ws = slot(w2c, w2s, t, g == 1)
+                        nc.tensor.matmul_mx(out=z[:, tt * HC:(tt + 1) * HC], lhsT=wc, lhsT_scale=ws,
+                                            rhs=half[g][0], rhs_scale=half[g][1],
+                                            start=(g == 0), stop=(g == 1))
+                for tt in range(2):
+                    t = 2 * q + tt
+                    nc.scalar.activation(out=rr[:, t * SL + CH:(t + 1) * SL], in_=z[:, tt * HC:(tt + 1) * HC],
+                                         func=ACT.Relu, bias=bc2[:, t:t + 1], scale=1.0)
+            rv = rr[:].rearrange("p (t i) -> p t i", t=4)
+            nc.vector.tensor_tensor(out=rv, in0=rv, in1=mb[:].unsqueeze(1).to_broadcast([P, 4, SL]), op=ALU.mult)
+            nc.vector.tensor_tensor(out=rv[0:H, :, 0:HC], in0=rv[0:H, :, 0:HC], in1=rv[0:H, :, CH:SL], op=ALU.max)
+            nc.vector.tensor_tensor(out=rv[H:P, :, HC:CH], in0=rv[H:P, :, HC:CH], in1=rv[H:P, :, CH:SL], op=ALU.max)
+            hg = work.tile([P, CH * 4], BF16, tag="hg", align_bytes=64)
+            nc.vector.tensor_copy(out=hg[:, 0:384 * 4].rearrange("p (c i t) -> p c t i", i=4, t=4),
+                                  in_=rv[:, :, 0:384].rearrange("p t (c i) -> p c t i", i=4))
+            nc.scalar.copy(out=hg[:, 384 * 4:CH * 4].rearrange("p (c i t) -> p c t i", i=4, t=4),
+                           in_=rv[:, :, 384:CH].rearrange("p t (c i) -> p c t i", i=4))
+            hc = work.tile([P, CH], U32, tag="hc", align_bytes=64)
+            hs = work.tile([P, CH], U8, tag="hs", align_bytes=64)
+            nc.vector.quantize_mx(out=hc[:].bitcast(FP8X4), scales=hs[:], in_=hg[:])
+            state[("h", c)] = (hc, hs)
+
+        out_view = out.rearrange("(s p r) d -> s p (r d)", p=P, r=SUP // P)
+
+        def back(c):
+            s, h = c // 2, c % 2
+            hc, hs = state[("h", c)]
+            osb = opool.tile([P, 4 * D], F32, tag="osb")
+            for r in range(4):
+                wc, ws = wfq[r // 2]
+                y = ps_y.tile([P, D], F32, tag="y")
+                nc.tensor.matmul_mx(out=y[:], lhsT=hc[:, r * P:(r + 1) * P].bitcast(FP8X4),
+                                    lhsT_scale=hs[:, r * P:(r + 1) * P],
+                                    rhs=wc[:].bitcast(FP8X4), rhs_scale=ws[:], start=True, stop=True)
+                nc.vector.tensor_tensor(out=osb[:, r * D:(r + 1) * D], in0=y[:], in1=bfb[:], op=ALU.add)
+            pieces = 4 if c == NCH - 1 else 1
+            w = 4 * D // pieces
+            for e in range(pieces):
+                nc.sync.dma_start(out=out_view[s][:, h * 4 * D + e * w:h * 4 * D + (e + 1) * w],
+                                  in_=osb[:, e * w:(e + 1) * w])
+
+        for c in range(NCH + 2):
+            if c >= 2:
+                back(c - 2)
+            if c < NCH:
+                front(c)
+            if c == 0:
+                prepare_wf()
+            if 1 <= c <= NCH:
+                mid(c - 1)

@@ -5,6 +5,7 @@ from concourse.masks import make_identity
 
 F32 = mybir.dt.float32
 BF16 = mybir.dt.bfloat16
+I32 = mybir.dt.int32
 U32 = mybir.dt.uint32
 U8 = mybir.dt.uint8
 FP8X4 = mybir.dt.float8_e4m3fn_x4
@@ -28,25 +29,27 @@ def tile_dynamiclayer_t_kernel(tc, x, W1, b1, W2, b2, Wf, bf, out):
     with ExitStack() as ctx:
         const = ctx.enter_context(tc.tile_pool(name="const", bufs=1))
         xpool = ctx.enter_context(tc.tile_pool(name="xpool", bufs=1))
-        work = ctx.enter_context(tc.tile_pool(name="work", bufs=2))
+        work = ctx.enter_context(tc.tile_pool(name="work", bufs=3))
         opool = ctx.enter_context(tc.tile_pool(name="opool", bufs=3))
         ps_x = ctx.enter_context(tc.psum_pool(name="ps_x", bufs=2))
         ps_z = ctx.enter_context(tc.psum_pool(name="ps_z", bufs=3))
         ps_y = ctx.enter_context(tc.psum_pool(name="ps_y", bufs=2))
         ps_m = ctx.enter_context(tc.psum_pool(name="ps_m", bufs=1))
+        ctx.enter_context(tc.manual_schedule())
 
         w1_sb = const.tile([P, 4 * D], BF16)
         w2_sb = const.tile([P, 4 * D], BF16)
         wf_sb = const.tile([P, 4 * 2 * U1], BF16)
-        nc.vector.memset(w2_sb[H:P, :], 0.0)
         nc.sync.dma_start(out=w1_sb[:], in_=W1.rearrange("(m t) k -> m (t k)", t=4))
-        nc.sync.dma_start(out=w2_sb[0:H, :], in_=W2.rearrange("(m t) k -> m (t k)", t=4))
         x_view = x.rearrange("(s p r) k -> s p (r k)", p=P, r=SUP // P)
         xs = []
         for s in range(NSUP):
             xt_sb = xpool.tile([P, (SUP // P) * D], BF16, name="x%d" % s)
             xs.append(xt_sb)
-        nc.sync.dma_start(out=xs[0][:], in_=x_view[0])
+        nc.sync.dma_start(out=xs[0][:, 0:4 * D], in_=x_view[0][:, 0:4 * D])
+        nc.vector.memset(w2_sb[H:P, :], 0.0)
+        nc.sync.dma_start(out=w2_sb[0:H, :], in_=W2.rearrange("(m t) k -> m (t k)", t=4))
+        nc.sync.dma_start(out=xs[0][:, 4 * D:8 * D], in_=x_view[0][:, 4 * D:8 * D])
         wf_dst = wf_sb[:].rearrange("p (a h u) -> p a h u", a=4, h=2)
         for h in range(2):
             nc.sync.dma_start(out=wf_dst[:, :, h, :], in_=Wf.rearrange("(a p) u -> p a u", p=P))
@@ -69,171 +72,284 @@ def tile_dynamiclayer_t_kernel(tc, x, W1, b1, W2, b2, Wf, bf, out):
 
         ident_f = const.tile([P, P], F32)
         make_identity(nc, ident_f[:])
-        ident_b = const.tile([P, P], BF16)
-        make_identity(nc, ident_b[:])
+        ones = const.tile([P, P], BF16)
+        nc.gpsimd.memset(ones[:], 1.0)
+        minus_d = const.tile([P, 1], F32)
+        nc.gpsimd.memset(minus_d[:], -float(D))
 
         bc1 = const.tile([P, 4], F32)
         bc1r = const.tile([P, 4], F32)
         bc2 = const.tile([P, 4], F32)
-        nc.vector.tensor_copy(out=bc1[:], in_=bb1[:])
-        nc.vector.tensor_copy(out=bc1r[:], in_=bb1r[:])
-        nc.vector.tensor_copy(out=bc2[:], in_=bb2[:])
+        nc.gpsimd.tensor_copy(out=bc1[:], in_=bb1[:])
+        nc.gpsimd.tensor_copy(out=bc1r[:], in_=bb1r[:])
+        nc.gpsimd.tensor_copy(out=bc2[:], in_=bb2[:])
 
-        def bank_of_transposes(srcs, dsts, copy_engine):
-            xt = ps_x.tile([P, 512], F32, tag="xt")
+        def transposes(bank, srcs):
             for n in range(4):
-                nc.tensor.transpose(xt[:, n * P:(n + 1) * P], srcs[n], ident_f[:])
-            src = xt[:].rearrange("p (r u j) -> p r j u", r=2, u=2)
-            for dst in dsts:
-                if copy_engine == "s":
-                    nc.scalar.copy(out=dst, in_=src)
-                else:
-                    nc.vector.tensor_copy(out=dst, in_=src)
+                nc.tensor.transpose(bank[:, n * P:(n + 1) * P], srcs[n], ident_f[:])
 
-        def halves(src_f32, tile_index):
-            base = tile_index * 256
-            return [src_f32[:, base:base + 2 * P:2], src_f32[:, base + 1:base + 2 * P:2]]
+        def empty(bank, dst, engine):
+            src = bank[:].rearrange("p (r u j) -> p r j u", r=2, u=2)
+            if engine == "s":
+                nc.scalar.copy(out=dst, in_=src)
+            else:
+                nc.vector.tensor_copy(out=dst, in_=src)
 
-        def stationary(w_sb, engine):
-            g = const.tile([P, 4 * 2 * P * 4], BF16, align_bytes=64, name="g_" + engine)
-            codes = const.tile([P, 4 * 2 * P], U32, align_bytes=64, name="c_" + engine)
-            scales = const.tile([P, 4 * 2 * P], U8, align_bytes=64, name="s_" + engine)
-            gv = g[:].bitcast(F32).rearrange("p (t d j u) -> p t d j u", t=4, d=2, u=2)
+        def words(view_f32, tile_index):
+            lo = tile_index * 256
+            return [view_f32[:, lo:lo + 256:2], view_f32[:, lo + 1:lo + 256:2]]
+
+        def stationary_transposes(w_sb, pool, tag):
             wv = w_sb[:].bitcast(F32)
+            banks = []
             for q in range(2):
-                bank_of_transposes(halves(wv, 2 * q) + halves(wv, 2 * q + 1),
-                                   [gv[:, 2 * q:2 * q + 2, 0], gv[:, 2 * q:2 * q + 2, 1]], engine)
+                bank = pool.tile([P, 512], F32, tag=tag, name="bank")
+                transposes(bank, words(wv, 2 * q) + words(wv, 2 * q + 1))
+                banks.append(bank)
+            return banks
+
+        def stationary_empty(banks, name, engines):
+            g = const.tile([P, 4 * P * 4], BF16, align_bytes=64, name="g_" + name)
+            gv = g[:].bitcast(F32).rearrange("p (t j u) -> p t j u", t=4, u=2)
+            for q in range(2):
+                empty(banks[q], gv[:, 2 * q:2 * q + 2], engines[q])
+            return g
+
+        def stationary_quantize(g, name):
+            codes = const.tile([P, 4 * P], U32, align_bytes=64, name="c_" + name)
+            scales = const.tile([P, 4 * P], U8, align_bytes=64, name="s_" + name)
             nc.vector.quantize_mx(out=codes[:].bitcast(FP8X4), scales=scales[:], in_=g[:])
             return codes, scales
 
-        w1c, w1s = stationary(w1_sb, "v")
-        w2c, w2s = stationary(w2_sb, "s")
+        def stationary_swap(codes, scales, name):
+            codes_r = const.tile([P, 4 * P], U32, align_bytes=64, name="cr_" + name)
+            scales_r = const.tile([P, 4 * P], U8, align_bytes=64, name="sr_" + name)
+            cv = codes[:].bitcast(I32).rearrange("p (t h j) -> p t h j", t=4, h=2)
+            crv = codes_r[:].bitcast(I32).rearrange("p (t h j) -> p t h j", t=4, h=2)
+            sv = scales[:].rearrange("p (t h j) -> p t h j", t=4, h=2)
+            srv = scales_r[:].rearrange("p (t h j) -> p t h j", t=4, h=2)
+            for h in range(2):
+                nc.vector.tensor_copy(out=crv[:, :, h, :], in_=cv[:, :, 1 - h, :])
+                nc.vector.tensor_copy(out=srv[:, :, h, :], in_=sv[:, :, 1 - h, :])
+            return codes_r, scales_r
 
-        def slot(codes, scales, t, shifted):
-            lo = t * 2 * P + (H if shifted else 0)
-            return codes[:, lo:lo + P].bitcast(FP8X4), scales[:, lo:lo + P]
+        def slot(pair, t):
+            return pair[0][:, t * P:(t + 1) * P].bitcast(FP8X4), pair[1][:, t * P:(t + 1) * P]
 
         wfq = []
 
-        def prepare_wf():
+        def prepare_wf(shifted):
             wv = wf_sb[:].bitcast(F32)
-            for shifted in range(2):
-                g = const.tile([P, D * 4], BF16, align_bytes=64, name="wfg%d" % shifted)
-                codes = const.tile([P, D], U32, align_bytes=64, name="wfc%d" % shifted)
-                scales = const.tile([P, D], U8, align_bytes=64, name="wfs%d" % shifted)
-                gv = g[:].bitcast(F32).rearrange("p (a j u) -> p a j u", a=4, u=2)
-                for q in range(2):
-                    srcs = []
-                    for a in (2 * q, 2 * q + 1):
-                        for u in range(2):
-                            lo = a * 512 + shifted * P + u
-                            srcs.append(wv[:, lo:lo + 256:2])
-                    bank_of_transposes(srcs, [gv[:, 2 * q:2 * q + 2]], "v")
-                nc.vector.quantize_mx(out=codes[:].bitcast(FP8X4), scales=scales[:], in_=g[:])
-                wfq.append((codes, scales))
+            g = const.tile([P, D * 4], BF16, align_bytes=64, name="wfg%d" % shifted)
+            codes = const.tile([P, D], U32, align_bytes=64, name="wfc%d" % shifted)
+            scales = const.tile([P, D], U8, align_bytes=64, name="wfs%d" % shifted)
+            gv = g[:].bitcast(F32).rearrange("p (a j u) -> p a j u", a=4, u=2)
+            for q in range(2):
+                srcs = []
+                for a in (2 * q, 2 * q + 1):
+                    for u in range(2):
+                        lo = a * 512 + shifted * P + u
+                        srcs.append(wv[:, lo:lo + 256:2])
+                bank = ps_y.tile([P, D], F32, tag="y", name="bank")
+                transposes(bank, srcs)
+                empty(bank, gv[:, 2 * q:2 * q + 2], "v")
+            nc.vector.quantize_mx(out=codes[:].bitcast(FP8X4), scales=scales[:], in_=g[:])
+            wfq.append((codes, scales))
 
         state = {}
 
-        def front(c):
+        def x_transposes(c):
             s, h = c // 2, c % 2
-            xc_sb = xs[s][:, h * 4 * D:(h + 1) * 4 * D]
-            ssum = work.tile([P, 4], F32, tag="ssum")
-            for r in range(4):
-                junk = work.tile([P, D], BF16, tag="junk")
-                nc.scalar.activation(out=junk[:], in_=xc_sb[:, r * D:(r + 1) * D], func=ACT.Abs,
-                                     accum_out=ssum[:, r:r + 1])
-            mcol = work.tile([P, 4], BF16, tag="mcol")
-            nc.gpsimd.tensor_scalar(out=mcol[:], in0=ssum[:], scalar1=float(D), scalar2=None,
-                                    op0=ALU.is_gt)
-            nl = work.tile([P, 2 * P], BF16, tag="nl")
-            nc.gpsimd.tensor_scalar(
-                out=nl[:].rearrange("p (r h c) -> p r h c", r=2, h=2),
-                in0=ssum[:].rearrange("p (h r) -> p r h", h=2).unsqueeze(3).to_broadcast([P, 2, 2, H]),
-                scalar1=float(D), scalar2=None, op0=ALU.is_le)
+            xv = xs[s][:, h * 4 * D:(h + 1) * 4 * D].bitcast(F32)
+            banks = []
+            for q in range(2):
+                bank = ps_x.tile([P, 512], F32, tag="xt", name="bank")
+                transposes(bank, words(xv, 2 * q) + words(xv, 2 * q + 1))
+                banks.append(bank)
+            state[("t", c)] = banks
+
+        def x_empty(c, engines):
             xg = work.tile([P, CH * 4], BF16, tag="xg", align_bytes=64)
             gv = xg[:].bitcast(F32).rearrange("p (r j u) -> p r j u", r=4, u=2)
-            xv = xc_sb.bitcast(F32)
             for q in range(2):
-                bank_of_transposes(halves(xv, 2 * q) + halves(xv, 2 * q + 1), [gv[:, 2 * q:2 * q + 2]], "s")
+                empty(state[("t", c)][q], gv[:, 2 * q:2 * q + 2], engines[q])
+            state[("g", c)] = xg
+
+        def x_abs(c):
+            xg = state[("g", c)]
+            xa = work.tile([P, CH * 4], BF16, tag="xa")
+            nc.vector.tensor_scalar(out=xa[:].bitcast(I32), in0=xg[:].bitcast(I32), scalar1=0x7FFF7FFF,
+                                    scalar2=None, op0=ALU.bitwise_and)
+            state[("a", c)] = xa
+
+        def x_quantize(c):
             xc = work.tile([P, CH], U32, tag="xc", align_bytes=64)
             xsc = work.tile([P, CH], U8, tag="xsc", align_bytes=64)
-            nc.vector.quantize_mx(out=xc[:].bitcast(FP8X4), scales=xsc[:], in_=xg[:])
-            state[("x", c)] = (xc, xsc, mcol, nl)
+            nc.vector.quantize_mx(out=xc[:].bitcast(FP8X4), scales=xsc[:], in_=state[("g", c)][:])
+            state[("x", c)] = [(xc[:, g * HC:(g + 1) * HC].bitcast(FP8X4), xsc[:, g * HC:(g + 1) * HC])
+                               for g in range(2)]
 
-        def mid(c):
-            xc, xsc, mcol, nl = state[("x", c)]
-            mb = ps_m.tile([P, CH + HC], BF16, tag="mb")
-            for r in range(4):
-                nc.tensor.matmul(out=mb[:, r * P:(r + 1) * P], lhsT=mcol[:, r:r + 1].to_broadcast([P, P]),
-                                 rhs=ident_b[:], start=True, stop=True)
-            for r in range(2):
-                nc.tensor.matmul(out=mb[:, CH + r * P:CH + (r + 1) * P], lhsT=nl[:, r * P:(r + 1) * P],
-                                 rhs=ident_b[:], start=True, stop=True)
-            half = [(xc[:, g * HC:(g + 1) * HC].bitcast(FP8X4), xsc[:, g * HC:(g + 1) * HC]) for g in range(2)]
-            rr = work.tile([P, 4 * SL], BF16, tag="rr")
+        def row_sums(c):
+            sm = ps_m.tile([P, CH], F32, tag="sm")
+            av = state[("a", c)][:].rearrange("p (i t) -> p i t", t=4)
             for t in range(4):
-                z = ps_z.tile([P, CH], F32, tag="z")
+                nc.tensor.matmul(out=sm[:], lhsT=ones[:], rhs=av[:, :, t], start=(t == 0), stop=(t == 3))
+            state[("s", c)] = sm
+
+        def sign(c):
+            sg = work.tile([P, CH], BF16, tag="sg")
+            nc.scalar.activation(out=sg[:], in_=state[("s", c)][:], func=ACT.Sign, bias=minus_d[:], scale=1.0)
+            state[("sg", c)] = sg
+
+        def masks(c):
+            sg = state[("sg", c)]
+            mb = work.tile([P, SL], BF16, tag="mb")
+            nc.vector.tensor_scalar(out=mb[:, 0:CH], in0=sg[:], scalar1=0.0, scalar2=None, op0=ALU.is_gt)
+            nc.vector.tensor_scalar(out=mb[0:H, CH:SL], in0=sg[0:H, 0:HC], scalar1=0.0, scalar2=None, op0=ALU.is_le)
+            nc.vector.tensor_scalar(out=mb[H:P, CH:SL], in0=sg[H:P, HC:CH], scalar1=0.0, scalar2=None, op0=ALU.is_le)
+            state[("m", c)] = mb
+
+        def long_z(c, t):
+            half = state[("x", c)]
+            z = ps_z.tile([P, CH], F32, tag="z")
+            for g in range(2):
+                wc, ws = slot(w1q[g], t)
+                nc.tensor.matmul_mx(out=z[:, g * HC:(g + 1) * HC], lhsT=wc, lhsT_scale=ws,
+                                    rhs=half[g][0], rhs_scale=half[g][1], start=True, stop=True)
+            state[("z", c, t)] = z
+
+        def short_z(c, q):
+            half = state[("x", c)]
+            z = ps_z.tile([P, CH], F32, tag="z")
+            for tt in range(2):
                 for g in range(2):
-                    wc, ws = slot(w1c, w1s, t, g == 1)
-                    nc.tensor.matmul_mx(out=z[:, g * HC:(g + 1) * HC], lhsT=wc, lhsT_scale=ws,
-                                        rhs=half[g][0], rhs_scale=half[g][1], start=True, stop=True)
-                for g in range(2):
-                    bias = bc1r if g == 1 else bc1
-                    nc.scalar.activation(out=rr[:, t * SL + g * HC:t * SL + (g + 1) * HC],
-                                         in_=z[:, g * HC:(g + 1) * HC], func=ACT.Relu,
-                                         bias=bias[:, t:t + 1], scale=1.0)
-            for q in range(2):
-                z = ps_z.tile([P, CH], F32, tag="z")
-                for tt in range(2):
-                    t = 2 * q + tt
-                    for g in range(2):
-                        wc, ws = slot(w2c, w2s, t, g == 1)
-                        nc.tensor.matmul_mx(out=z[:, tt * HC:(tt + 1) * HC], lhsT=wc, lhsT_scale=ws,
-                                            rhs=half[g][0], rhs_scale=half[g][1],
-                                            start=(g == 0), stop=(g == 1))
-                for tt in range(2):
-                    t = 2 * q + tt
-                    nc.scalar.activation(out=rr[:, t * SL + CH:(t + 1) * SL], in_=z[:, tt * HC:(tt + 1) * HC],
-                                         func=ACT.Relu, bias=bc2[:, t:t + 1], scale=1.0)
-            rv = rr[:].rearrange("p (t i) -> p t i", t=4)
-            nc.vector.tensor_tensor(out=rv, in0=rv, in1=mb[:].unsqueeze(1).to_broadcast([P, 4, SL]), op=ALU.mult)
+                    wc, ws = slot(w2q[g], 2 * q + tt)
+                    nc.tensor.matmul_mx(out=z[:, tt * HC:(tt + 1) * HC], lhsT=wc, lhsT_scale=ws,
+                                        rhs=half[g][0], rhs_scale=half[g][1], start=(g == 0), stop=(g == 1))
+            state[("z", c, 4 + q)] = z
+
+        def relu(c, n):
+            if n == 0:
+                rr = work.tile([P, 4 * SL], BF16, tag="rr")
+                state[("r", c)] = rr
+            rr = state[("r", c)]
+            z = state[("z", c, n)]
+            for g in range(2):
+                if n < 4:
+                    t, lo, n_cols, bias = n, g * HC, HC, (bc1, bc1r)[g]
+                else:
+                    t, lo, n_cols, bias = 2 * (n - 4) + g, CH, HC, bc2
+                nc.scalar.activation(out=rr[:, t * SL + lo:t * SL + lo + n_cols], in_=z[:, g * HC:(g + 1) * HC],
+                                     func=ACT.Relu, bias=bias[:, t:t + 1], scale=1.0)
+
+        def mask_multiply(c):
+            rv = state[("r", c)][:].rearrange("p (t i) -> p t i", t=4)
+            nc.vector.tensor_tensor(out=rv, in0=rv, in1=state[("m", c)][:].unsqueeze(1).to_broadcast([P, 4, SL]),
+                                    op=ALU.mult)
+
+        def merge(c):
+            rv = state[("r", c)][:].rearrange("p (t i) -> p t i", t=4)
             nc.vector.tensor_tensor(out=rv[0:H, :, 0:HC], in0=rv[0:H, :, 0:HC], in1=rv[0:H, :, CH:SL], op=ALU.max)
             nc.vector.tensor_tensor(out=rv[H:P, :, HC:CH], in0=rv[H:P, :, HC:CH], in1=rv[H:P, :, CH:SL], op=ALU.max)
+
+        def regroup(c):
+            rv = state[("r", c)][:].rearrange("p (t i) -> p t i", t=4)
             hg = work.tile([P, CH * 4], BF16, tag="hg", align_bytes=64)
-            nc.vector.tensor_copy(out=hg[:, 0:384 * 4].rearrange("p (c i t) -> p c t i", i=4, t=4),
-                                  in_=rv[:, :, 0:384].rearrange("p t (c i) -> p c t i", i=4))
-            nc.scalar.copy(out=hg[:, 384 * 4:CH * 4].rearrange("p (c i t) -> p c t i", i=4, t=4),
-                           in_=rv[:, :, 384:CH].rearrange("p t (c i) -> p c t i", i=4))
+            nc.scalar.copy(out=hg[:].rearrange("p (c i t) -> p c t i", i=4, t=4),
+                           in_=rv[:, :, 0:CH].rearrange("p t (c i) -> p c t i", i=4))
+            state[("hg", c)] = hg
+
+        def h_quantize(c):
             hc = work.tile([P, CH], U32, tag="hc", align_bytes=64)
             hs = work.tile([P, CH], U8, tag="hs", align_bytes=64)
-            nc.vector.quantize_mx(out=hc[:].bitcast(FP8X4), scales=hs[:], in_=hg[:])
+            nc.vector.quantize_mx(out=hc[:].bitcast(FP8X4), scales=hs[:], in_=state[("hg", c)][:])
             state[("h", c)] = (hc, hs)
 
         out_view = out.rearrange("(s p r) d -> s p (r d)", p=P, r=SUP // P)
 
-        def back(c):
-            s, h = c // 2, c % 2
+        def last_matmul(c, r):
             hc, hs = state[("h", c)]
-            osb = opool.tile([P, 4 * D], F32, tag="osb")
-            for r in range(4):
-                wc, ws = wfq[r // 2]
-                y = ps_y.tile([P, D], F32, tag="y")
-                nc.tensor.matmul_mx(out=y[:], lhsT=hc[:, r * P:(r + 1) * P].bitcast(FP8X4),
-                                    lhsT_scale=hs[:, r * P:(r + 1) * P],
-                                    rhs=wc[:].bitcast(FP8X4), rhs_scale=ws[:], start=True, stop=True)
-                nc.vector.tensor_tensor(out=osb[:, r * D:(r + 1) * D], in0=y[:], in1=bfb[:], op=ALU.add)
-            pieces = 4 if c == NCH - 1 else 1
-            w = 4 * D // pieces
-            for e in range(pieces):
-                nc.sync.dma_start(out=out_view[s][:, h * 4 * D + e * w:h * 4 * D + (e + 1) * w],
-                                  in_=osb[:, e * w:(e + 1) * w])
+            wc, ws = wfq[r // 2]
+            y = ps_y.tile([P, D], F32, tag="y")
+            nc.tensor.matmul_mx(out=y[:], lhsT=hc[:, r * P:(r + 1) * P].bitcast(FP8X4),
+                                lhsT_scale=hs[:, r * P:(r + 1) * P],
+                                rhs=wc[:].bitcast(FP8X4), rhs_scale=ws[:], start=True, stop=True)
+            state[("y", c, r)] = y
 
-        for c in range(NCH + 2):
-            if c >= 2:
-                back(c - 2)
-            if c < NCH:
-                front(c)
-            if c == 0:
-                prepare_wf()
-            if 1 <= c <= NCH:
-                mid(c - 1)
+        def add_and_store(c, r):
+            s, h = c // 2, c % 2
+            if r == 0:
+                osb = opool.tile([P, 4 * D], F32, tag="osb")
+                state[("o", c)] = osb
+            osb = state[("o", c)]
+            nc.vector.tensor_tensor(out=osb[:, r * D:(r + 1) * D], in0=state[("y", c, r)][:], in1=bfb[:], op=ALU.add)
+            last = c == NCH - 1
+            if last or r == 3:
+                lo = r * D if last else 0
+                nc.sync.dma_start(out=out_view[s][:, h * 4 * D + lo:h * 4 * D + (r + 1) * D],
+                                  in_=osb[:, lo:(r + 1) * D])
+
+        banks1 = stationary_transposes(w1_sb, ps_z, "z")
+        g1 = stationary_empty(banks1, "w1", "sv")
+        x_transposes(0)
+        pair1 = stationary_quantize(g1, "w1")
+        x_empty(0, "sv")
+        banks2 = stationary_transposes(w2_sb, ps_y, "y")
+        x_quantize(0)
+        w1q = [pair1, stationary_swap(pair1[0], pair1[1], "w1")]
+        x_abs(0)
+        g2 = stationary_empty(banks2, "w2", "ss")
+        pair2 = stationary_quantize(g2, "w2")
+        w2q = [pair2, stationary_swap(pair2[0], pair2[1], "w2")]
+        x_transposes(1)
+
+        for i in range(NCH + 2):
+            now, nxt = i < NCH, i + 1 < NCH
+            sel, fin = 0 <= i - 1 < NCH, 0 <= i - 2 < NCH
+            if sel:
+                mask_multiply(i - 1)
+            if fin:
+                h_quantize(i - 2)
+            if sel:
+                merge(i - 1)
+            if nxt:
+                x_empty(i + 1, "ss")
+            if now:
+                for n in range(3):
+                    long_z(i, n)
+                if i == 0:
+                    row_sums(0)
+                if i + 2 < NCH:
+                    x_transposes(i + 2)
+                for n in range(3):
+                    relu(i, n)
+                long_z(i, 3)
+                short_z(i, 0)
+                short_z(i, 1)
+                if i == 0:
+                    sign(0)
+                for n in range(3, 6):
+                    relu(i, n)
+                masks(i)
+            if nxt:
+                x_abs(i + 1)
+                x_quantize(i + 1)
+            if fin:
+                last_matmul(i - 2, 0)
+                last_matmul(i - 2, 1)
+            if nxt:
+                row_sums(i + 1)
+            if fin:
+                add_and_store(i - 2, 0)
+                last_matmul(i - 2, 2)
+                add_and_store(i - 2, 1)
+                last_matmul(i - 2, 3)
+                add_and_store(i - 2, 2)
+                add_and_store(i - 2, 3)
+            if i == 0:
+                prepare_wf(0)
+                prepare_wf(1)
+            if sel:
+                regroup(i - 1)
+            if nxt:
+                sign(i + 1)

@@ -13,15 +13,15 @@ ALU = mybir.AluOpType
 ACT = mybir.ActivationFunctionType
 
 P = 128
-H = 64
 B, D, U1, U2 = 8192, 512, 512, 256
 FLOPS = 2 * B * D * (U1 + U2) + 2 * B * U1 * D
 CH = 512
-HC = CH // 2
-SL = CH + HC
+R = CH // P
 NCH = B // CH
 SUP = 1024
 NSUP = B // SUP
+ROWS = U1 + D + U2
+OFF = -3.0e38
 
 
 def tile_dynamiclayer_t_kernel(tc, x, W1, b1, W2, b2, Wf, bf, out):
@@ -31,58 +31,39 @@ def tile_dynamiclayer_t_kernel(tc, x, W1, b1, W2, b2, Wf, bf, out):
         xpool = ctx.enter_context(tc.tile_pool(name="xpool", bufs=1))
         work = ctx.enter_context(tc.tile_pool(name="work", bufs=3))
         opool = ctx.enter_context(tc.tile_pool(name="opool", bufs=3))
-        ps_x = ctx.enter_context(tc.psum_pool(name="ps_x", bufs=2))
-        ps_z = ctx.enter_context(tc.psum_pool(name="ps_z", bufs=3))
+        ps_t = ctx.enter_context(tc.psum_pool(name="ps_t", bufs=3))
+        ps_z = ctx.enter_context(tc.psum_pool(name="ps_z", bufs=2))
+        ps_s = ctx.enter_context(tc.psum_pool(name="ps_s", bufs=1))
         ps_y = ctx.enter_context(tc.psum_pool(name="ps_y", bufs=2))
-        ps_m = ctx.enter_context(tc.psum_pool(name="ps_m", bufs=1))
         ctx.enter_context(tc.manual_schedule())
 
-        w1_sb = const.tile([P, 4 * D], BF16)
-        w2_sb = const.tile([P, 4 * D], BF16)
-        wf_sb = const.tile([P, 4 * 2 * U1], BF16)
-        nc.sync.dma_start(out=w1_sb[:], in_=W1.rearrange("(m t) k -> m (t k)", t=4))
+        w1_sb = const.tile([P, 4, D], BF16)
+        w2_sb = const.tile([P, 2, D], BF16)
+        wf_sb = const.tile([P, 4, U1], BF16)
+        rows = const.tile([P, ROWS], BF16)
+        warm = const.tile([P, 1], F32)
+        nc.vector.memset(rows[:].bitcast(I32), 0)
+        nc.vector.memset(warm[:], 0.0)
+        nc.scalar.activation(out=warm[:], in_=warm[:], func=ACT.Relu)
+        nc.scalar.dma_start(out=rows[0:1, 2 * D:ROWS], in_=b2.unsqueeze(0))
+        nc.scalar.dma_start(out=rows[0:1, 0:D], in_=b1.unsqueeze(0))
+        nc.scalar.dma_start(out=rows[0:1, D:2 * D], in_=bf.unsqueeze(0))
         x_view = x.rearrange("(s p r) k -> s p (r k)", p=P, r=SUP // P)
         xs = []
         for s in range(NSUP):
             xt_sb = xpool.tile([P, (SUP // P) * D], BF16, name="x%d" % s)
             xs.append(xt_sb)
+        nc.sync.dma_start(out=w1_sb[:], in_=W1.rearrange("(a p) k -> p a k", p=P))
         nc.sync.dma_start(out=xs[0][:, 0:4 * D], in_=x_view[0][:, 0:4 * D])
-        nc.vector.memset(w2_sb[H:P, :], 0.0)
-        nc.sync.dma_start(out=w2_sb[0:H, :], in_=W2.rearrange("(m t) k -> m (t k)", t=4))
+        nc.sync.dma_start(out=w2_sb[:], in_=W2.rearrange("(a p) k -> p a k", p=P))
         nc.sync.dma_start(out=xs[0][:, 4 * D:8 * D], in_=x_view[0][:, 4 * D:8 * D])
-        wf_dst = wf_sb[:].rearrange("p (a h u) -> p a h u", a=4, h=2)
-        for h in range(2):
-            nc.sync.dma_start(out=wf_dst[:, :, h, :], in_=Wf.rearrange("(a p) u -> p a u", p=P))
+        nc.sync.dma_start(out=wf_sb[:], in_=Wf.rearrange("(a p) u -> p a u", p=P))
         for s in range(1, NSUP):
             nc.sync.dma_start(out=xs[s][:], in_=x_view[s])
-
-        bb1 = const.tile([P, 4], BF16)
-        bb1r = const.tile([P, 4], BF16)
-        bb2 = const.tile([P, 4], BF16)
-        b1v = b1.rearrange("(p t) -> p t", t=4)
-        b2v = b2.rearrange("(p t) -> p t", t=4)
-        with nc.allow_non_contiguous_dma(reason="four bias values to a partition"):
-            nc.scalar.dma_start(out=bb1[:], in_=b1v)
-            nc.scalar.dma_start(out=bb1r[0:H, :], in_=b1v[H:P, :])
-            nc.scalar.dma_start(out=bb1r[H:P, :], in_=b1v[0:H, :])
-            nc.scalar.dma_start(out=bb2[0:H, :], in_=b2v)
-            nc.scalar.dma_start(out=bb2[H:P, :], in_=b2v)
-        bfb = const.tile([P, D], BF16)
-        nc.gpsimd.dma_start(out=bfb[:], in_=bf.partition_broadcast(P))
-
         ident_f = const.tile([P, P], F32)
         make_identity(nc, ident_f[:])
         ones = const.tile([P, P], BF16)
         nc.gpsimd.memset(ones[:], 1.0)
-        minus_d = const.tile([P, 1], F32)
-        nc.gpsimd.memset(minus_d[:], -float(D))
-
-        bc1 = const.tile([P, 4], F32)
-        bc1r = const.tile([P, 4], F32)
-        bc2 = const.tile([P, 4], F32)
-        nc.gpsimd.tensor_copy(out=bc1[:], in_=bb1[:])
-        nc.gpsimd.tensor_copy(out=bc1r[:], in_=bb1r[:])
-        nc.gpsimd.tensor_copy(out=bc2[:], in_=bb2[:])
 
         def transposes(bank, srcs):
             for n in range(4):
@@ -95,66 +76,35 @@ def tile_dynamiclayer_t_kernel(tc, x, W1, b1, W2, b2, Wf, bf, out):
             else:
                 nc.vector.tensor_copy(out=dst, in_=src)
 
-        def words(view_f32, tile_index):
+        def words(flat_f32, tile_index):
             lo = tile_index * 256
-            return [view_f32[:, lo:lo + 256:2], view_f32[:, lo + 1:lo + 256:2]]
+            return [flat_f32[:, lo:lo + 256:2], flat_f32[:, lo + 1:lo + 256:2]]
 
-        def stationary_transposes(w_sb, pool, tag):
-            wv = w_sb[:].bitcast(F32)
-            banks = []
-            for q in range(2):
-                bank = pool.tile([P, 512], F32, tag=tag, name="bank")
-                transposes(bank, words(wv, 2 * q) + words(wv, 2 * q + 1))
-                banks.append(bank)
-            return banks
+        def weight_transposes(w_sb, q, pool, tag):
+            wv = w_sb[:].rearrange("p a k -> p (a k)").bitcast(F32)
+            bank = pool.tile([P, 512], F32, tag=tag, name="bank")
+            transposes(bank, words(wv, 2 * q) + words(wv, 2 * q + 1))
+            return bank
 
-        def stationary_empty(banks, name, engines):
-            g = const.tile([P, 4 * P * 4], BF16, align_bytes=64, name="g_" + name)
-            gv = g[:].bitcast(F32).rearrange("p (t j u) -> p t j u", t=4, u=2)
-            for q in range(2):
-                empty(banks[q], gv[:, 2 * q:2 * q + 2], engines[q])
-            return g
+        def weight_tile(units, name):
+            return const.tile([P, units * 4], BF16, align_bytes=64, name="g_" + name)
 
-        def stationary_quantize(g, name):
-            codes = const.tile([P, 4 * P], U32, align_bytes=64, name="c_" + name)
-            scales = const.tile([P, 4 * P], U8, align_bytes=64, name="s_" + name)
+        def weight_part(g, q):
+            gv = g[:].bitcast(F32).rearrange("p (a j u) -> p a j u", j=P, u=2)
+            return gv[:, 2 * q:2 * q + 2]
+
+        def weight_quantize(g, units, name):
+            codes = const.tile([P, units], U32, align_bytes=64, name="c_" + name)
+            scales = const.tile([P, units], U8, align_bytes=64, name="s_" + name)
             nc.vector.quantize_mx(out=codes[:].bitcast(FP8X4), scales=scales[:], in_=g[:])
-            return codes, scales
+            return codes[:].bitcast(FP8X4), scales[:]
 
-        def stationary_swap(codes, scales, name):
-            codes_r = const.tile([P, 4 * P], U32, align_bytes=64, name="cr_" + name)
-            scales_r = const.tile([P, 4 * P], U8, align_bytes=64, name="sr_" + name)
-            cv = codes[:].bitcast(I32).rearrange("p (t h j) -> p t h j", t=4, h=2)
-            crv = codes_r[:].bitcast(I32).rearrange("p (t h j) -> p t h j", t=4, h=2)
-            sv = scales[:].rearrange("p (t h j) -> p t h j", t=4, h=2)
-            srv = scales_r[:].rearrange("p (t h j) -> p t h j", t=4, h=2)
-            for h in range(2):
-                nc.vector.tensor_copy(out=crv[:, :, h, :], in_=cv[:, :, 1 - h, :])
-                nc.vector.tensor_copy(out=srv[:, :, h, :], in_=sv[:, :, 1 - h, :])
-            return codes_r, scales_r
-
-        def slot(pair, t):
-            return pair[0][:, t * P:(t + 1) * P].bitcast(FP8X4), pair[1][:, t * P:(t + 1) * P]
-
-        wfq = []
-
-        def prepare_wf(shifted):
-            wv = wf_sb[:].bitcast(F32)
-            g = const.tile([P, D * 4], BF16, align_bytes=64, name="wfg%d" % shifted)
-            codes = const.tile([P, D], U32, align_bytes=64, name="wfc%d" % shifted)
-            scales = const.tile([P, D], U8, align_bytes=64, name="wfs%d" % shifted)
-            gv = g[:].bitcast(F32).rearrange("p (a j u) -> p a j u", a=4, u=2)
-            for q in range(2):
-                srcs = []
-                for a in (2 * q, 2 * q + 1):
-                    for u in range(2):
-                        lo = a * 512 + shifted * P + u
-                        srcs.append(wv[:, lo:lo + 256:2])
-                bank = ps_y.tile([P, D], F32, tag="y", name="bank")
-                transposes(bank, srcs)
-                empty(bank, gv[:, 2 * q:2 * q + 2], "v")
-            nc.vector.quantize_mx(out=codes[:].bitcast(FP8X4), scales=scales[:], in_=g[:])
-            wfq.append((codes, scales))
+        def spread_row(lo, width, pool, tag, name):
+            bank = pool.tile([P, 512], F32, tag=tag, name="bank")
+            nc.tensor.matmul(out=bank[:, 0:width], lhsT=ones[:], rhs=rows[:, lo:lo + width], start=True, stop=True)
+            row = const.tile([P, width], BF16, name=name)
+            nc.scalar.copy(out=row[:], in_=bank[:, 0:width])
+            return row
 
         state = {}
 
@@ -163,7 +113,7 @@ def tile_dynamiclayer_t_kernel(tc, x, W1, b1, W2, b2, Wf, bf, out):
             xv = xs[s][:, h * 4 * D:(h + 1) * 4 * D].bitcast(F32)
             banks = []
             for q in range(2):
-                bank = ps_x.tile([P, 512], F32, tag="xt", name="bank")
+                bank = ps_t.tile([P, 512], F32, tag="t", name="bank")
                 transposes(bank, words(xv, 2 * q) + words(xv, 2 * q + 1))
                 banks.append(bank)
             state[("t", c)] = banks
@@ -175,88 +125,89 @@ def tile_dynamiclayer_t_kernel(tc, x, W1, b1, W2, b2, Wf, bf, out):
                 empty(state[("t", c)][q], gv[:, 2 * q:2 * q + 2], engines[q])
             state[("g", c)] = xg
 
-        def x_abs(c):
-            xg = state[("g", c)]
-            xa = work.tile([P, CH * 4], BF16, tag="xa")
-            nc.vector.tensor_scalar(out=xa[:].bitcast(I32), in0=xg[:].bitcast(I32), scalar1=0x7FFF7FFF,
-                                    scalar2=None, op0=ALU.bitwise_and)
-            state[("a", c)] = xa
-
         def x_quantize(c):
             xc = work.tile([P, CH], U32, tag="xc", align_bytes=64)
             xsc = work.tile([P, CH], U8, tag="xsc", align_bytes=64)
             nc.vector.quantize_mx(out=xc[:].bitcast(FP8X4), scales=xsc[:], in_=state[("g", c)][:])
-            state[("x", c)] = [(xc[:, g * HC:(g + 1) * HC].bitcast(FP8X4), xsc[:, g * HC:(g + 1) * HC])
-                               for g in range(2)]
+            state[("x", c)] = (xc, xsc)
 
         def row_sums(c):
-            sm = ps_m.tile([P, CH], F32, tag="sm")
-            av = state[("a", c)][:].rearrange("p (i t) -> p i t", t=4)
-            for t in range(4):
-                nc.tensor.matmul(out=sm[:], lhsT=ones[:], rhs=av[:, :, t], start=(t == 0), stop=(t == 3))
-            state[("s", c)] = sm
+            s, h = c // 2, c % 2
+            ssum = work.tile([P, R], F32, tag="ssum")
+            state[("s", c)] = ssum
+            for r in range(R):
+                junk = work.tile([P, D], BF16, tag="junk")
+                lo = (h * R + r) * D
+                nc.scalar.activation(out=junk[:], in_=xs[s][:, lo:lo + D], func=ACT.Abs, accum_out=ssum[:, r:r + 1])
 
-        def sign(c):
-            sg = work.tile([P, CH], BF16, tag="sg")
-            nc.scalar.activation(out=sg[:], in_=state[("s", c)][:], func=ACT.Sign, bias=minus_d[:], scale=1.0)
-            state[("sg", c)] = sg
+        def offsets(c):
+            ssum = state[("s", c)]
+            off1 = work.tile([P, R], F32, tag="off1")
+            off2 = work.tile([P, R], F32, tag="off2")
+            nc.gpsimd.tensor_scalar(out=off1[:], in0=ssum[:], scalar1=float(D), scalar2=OFF, op0=ALU.is_le, op1=ALU.mult)
+            nc.gpsimd.tensor_scalar(out=off2[:], in0=ssum[:], scalar1=float(D), scalar2=OFF, op0=ALU.is_gt, op1=ALU.mult)
+            state[("off", c)] = (off1, off2)
 
-        def masks(c):
-            sg = state[("sg", c)]
-            mb = work.tile([P, SL], BF16, tag="mb")
-            nc.vector.tensor_scalar(out=mb[:, 0:CH], in0=sg[:], scalar1=0.0, scalar2=None, op0=ALU.is_gt)
-            nc.vector.tensor_scalar(out=mb[0:H, CH:SL], in0=sg[0:H, 0:HC], scalar1=0.0, scalar2=None, op0=ALU.is_le)
-            nc.vector.tensor_scalar(out=mb[H:P, CH:SL], in0=sg[H:P, HC:CH], scalar1=0.0, scalar2=None, op0=ALU.is_le)
-            state[("m", c)] = mb
+        def x_tile(c, r):
+            xc, xsc = state[("x", c)]
+            return xc[:, r * P:(r + 1) * P].bitcast(FP8X4), xsc[:, r * P:(r + 1) * P]
 
-        def long_z(c, t):
-            half = state[("x", c)]
-            z = ps_z.tile([P, CH], F32, tag="z")
-            for g in range(2):
-                wc, ws = slot(w1q[g], t)
-                nc.tensor.matmul_mx(out=z[:, g * HC:(g + 1) * HC], lhsT=wc, lhsT_scale=ws,
-                                    rhs=half[g][0], rhs_scale=half[g][1], start=True, stop=True)
-            state[("z", c, t)] = z
+        def long_z(c, r):
+            z = ps_z.tile([P, U1], F32, tag="z")
+            xc, xsc = x_tile(c, r)
+            nc.tensor.matmul_mx(out=z[:], lhsT=xc, lhsT_scale=xsc, rhs=w1q[0], rhs_scale=w1q[1], start=True, stop=True)
+            state[("z", c, r)] = z
 
         def short_z(c, q):
-            half = state[("x", c)]
-            z = ps_z.tile([P, CH], F32, tag="z")
-            for tt in range(2):
-                for g in range(2):
-                    wc, ws = slot(w2q[g], 2 * q + tt)
-                    nc.tensor.matmul_mx(out=z[:, tt * HC:(tt + 1) * HC], lhsT=wc, lhsT_scale=ws,
-                                        rhs=half[g][0], rhs_scale=half[g][1], start=(g == 0), stop=(g == 1))
-            state[("z", c, 4 + q)] = z
+            z = ps_s.tile([P, 2 * U2], F32, tag="s")
+            for e in range(2):
+                xc, xsc = x_tile(c, 2 * q + e)
+                nc.tensor.matmul_mx(out=z[:, e * U2:(e + 1) * U2], lhsT=xc, lhsT_scale=xsc,
+                                    rhs=w2q[0], rhs_scale=w2q[1], start=True, stop=True)
+            state[("zs", c, q)] = z
 
-        def relu(c, n):
-            if n == 0:
-                rr = work.tile([P, 4 * SL], BF16, tag="rr")
-                state[("r", c)] = rr
-            rr = state[("r", c)]
-            z = state[("z", c, n)]
-            for g in range(2):
-                if n < 4:
-                    t, lo, n_cols, bias = n, g * HC, HC, (bc1, bc1r)[g]
-                else:
-                    t, lo, n_cols, bias = 2 * (n - 4) + g, CH, HC, bc2
-                nc.scalar.activation(out=rr[:, t * SL + lo:t * SL + lo + n_cols], in_=z[:, g * HC:(g + 1) * HC],
-                                     func=ACT.Relu, bias=bias[:, t:t + 1], scale=1.0)
+        def long_bias(c, r):
+            if r == 0:
+                h1 = work.tile([P, R * U1], BF16, tag="h1")
+                state[("h1", c)] = h1
+            nc.vector.scalar_tensor_tensor(out=state[("h1", c)][:, r * U1:(r + 1) * U1], in0=state[("z", c, r)][:],
+                                           scalar=state[("off", c)][0][:, r:r + 1], in1=b1_row[:],
+                                           op0=ALU.add, op1=ALU.add)
 
-        def mask_multiply(c):
-            rv = state[("r", c)][:].rearrange("p (t i) -> p t i", t=4)
-            nc.vector.tensor_tensor(out=rv, in0=rv, in1=state[("m", c)][:].unsqueeze(1).to_broadcast([P, 4, SL]),
-                                    op=ALU.mult)
+        def short_bias(c, r):
+            if r == 0:
+                h2 = work.tile([P, R * U2], BF16, tag="h2")
+                state[("h2", c)] = h2
+            e = r % 2
+            nc.vector.scalar_tensor_tensor(out=state[("h2", c)][:, r * U2:(r + 1) * U2],
+                                           in0=state[("zs", c, r // 2)][:, e * U2:(e + 1) * U2],
+                                           scalar=state[("off", c)][1][:, r:r + 1], in1=b2_row[:],
+                                           op0=ALU.add, op1=ALU.add)
 
         def merge(c):
-            rv = state[("r", c)][:].rearrange("p (t i) -> p t i", t=4)
-            nc.vector.tensor_tensor(out=rv[0:H, :, 0:HC], in0=rv[0:H, :, 0:HC], in1=rv[0:H, :, CH:SL], op=ALU.max)
-            nc.vector.tensor_tensor(out=rv[H:P, :, HC:CH], in0=rv[H:P, :, HC:CH], in1=rv[H:P, :, CH:SL], op=ALU.max)
+            low = state[("h1", c)][:].rearrange("p (r u) -> p r u", r=R)[:, :, 0:U2]
+            nc.vector.tensor_tensor(out=low, in0=low, in1=state[("h2", c)][:].rearrange("p (r u) -> p r u", r=R),
+                                    op=ALU.max)
 
-        def regroup(c):
-            rv = state[("r", c)][:].rearrange("p (t i) -> p t i", t=4)
+        def relu(c):
+            for q in range(2):
+                part = state[("h1", c)][:, q * 2 * U1:(q + 1) * 2 * U1]
+                nc.scalar.activation(out=part, in_=part, func=ACT.Relu)
+
+        def h_transposes(c):
+            hv = state[("h1", c)][:].bitcast(F32)
+            banks = []
+            for q in range(2):
+                bank = ps_t.tile([P, 512], F32, tag="t", name="bank")
+                transposes(bank, words(hv, 2 * q) + words(hv, 2 * q + 1))
+                banks.append(bank)
+            state[("ht", c)] = banks
+
+        def h_empty(c):
             hg = work.tile([P, CH * 4], BF16, tag="hg", align_bytes=64)
-            nc.scalar.copy(out=hg[:].rearrange("p (c i t) -> p c t i", i=4, t=4),
-                           in_=rv[:, :, 0:CH].rearrange("p t (c i) -> p c t i", i=4))
+            gv = hg[:].bitcast(F32).rearrange("p (r j u) -> p r j u", r=4, u=2)
+            for q in range(2):
+                empty(state[("ht", c)][q], gv[:, 2 * q:2 * q + 2], "s")
             state[("hg", c)] = hg
 
         def h_quantize(c):
@@ -269,87 +220,103 @@ def tile_dynamiclayer_t_kernel(tc, x, W1, b1, W2, b2, Wf, bf, out):
 
         def last_matmul(c, r):
             hc, hs = state[("h", c)]
-            wc, ws = wfq[r // 2]
             y = ps_y.tile([P, D], F32, tag="y")
             nc.tensor.matmul_mx(out=y[:], lhsT=hc[:, r * P:(r + 1) * P].bitcast(FP8X4),
                                 lhsT_scale=hs[:, r * P:(r + 1) * P],
-                                rhs=wc[:].bitcast(FP8X4), rhs_scale=ws[:], start=True, stop=True)
+                                rhs=wfq[0], rhs_scale=wfq[1], start=True, stop=True)
             state[("y", c, r)] = y
 
         def add_and_store(c, r):
             s, h = c // 2, c % 2
             if r == 0:
-                osb = opool.tile([P, 4 * D], F32, tag="osb")
+                osb = opool.tile([P, R * D], F32, tag="osb")
                 state[("o", c)] = osb
             osb = state[("o", c)]
-            nc.vector.tensor_tensor(out=osb[:, r * D:(r + 1) * D], in0=state[("y", c, r)][:], in1=bfb[:], op=ALU.add)
+            nc.vector.tensor_tensor(out=osb[:, r * D:(r + 1) * D], in0=state[("y", c, r)][:], in1=bf_row[:], op=ALU.add)
             last = c == NCH - 1
-            if last or r == 3:
+            if last or r == R - 1:
                 lo = r * D if last else 0
-                nc.sync.dma_start(out=out_view[s][:, h * 4 * D + lo:h * 4 * D + (r + 1) * D],
+                nc.sync.dma_start(out=out_view[s][:, h * R * D + lo:h * R * D + (r + 1) * D],
                                   in_=osb[:, lo:(r + 1) * D])
 
-        banks1 = stationary_transposes(w1_sb, ps_z, "z")
-        g1 = stationary_empty(banks1, "w1", "sv")
+        g1 = weight_tile(U1, "w1")
+        g2 = weight_tile(U2, "w2")
+        gf = weight_tile(U1, "wf")
+        w1_banks = [weight_transposes(w1_sb, q, ps_z, "z") for q in range(2)]
+        empty(w1_banks[0], weight_part(g1, 0), "s")
+        empty(w1_banks[1], weight_part(g1, 1), "v")
         x_transposes(0)
-        pair1 = stationary_quantize(g1, "w1")
+        w1q = weight_quantize(g1, U1, "w1")
         x_empty(0, "sv")
-        banks2 = stationary_transposes(w2_sb, ps_y, "y")
+        w2_bank = weight_transposes(w2_sb, 0, ps_s, "s")
+        row_sums(0)
+        offsets(0)
         x_quantize(0)
-        w1q = [pair1, stationary_swap(pair1[0], pair1[1], "w1")]
-        x_abs(0)
-        g2 = stationary_empty(banks2, "w2", "ss")
-        pair2 = stationary_quantize(g2, "w2")
-        w2q = [pair2, stationary_swap(pair2[0], pair2[1], "w2")]
+        empty(w2_bank, weight_part(g2, 0), "v")
+        w2q = weight_quantize(g2, U2, "w2")
+        b2_row = spread_row(2 * D, U2, ps_y, "y", "b2_row")
+        b1_row = spread_row(0, U1, ps_y, "y", "b1_row")
         x_transposes(1)
+        row_sums(1)
+        long_z(0, 0)
+        short_z(0, 0)
+        long_z(0, 1)
 
         for i in range(NCH + 2):
             now, nxt = i < NCH, i + 1 < NCH
-            sel, fin = 0 <= i - 1 < NCH, 0 <= i - 2 < NCH
-            if sel:
-                mask_multiply(i - 1)
-            if fin:
-                h_quantize(i - 2)
-            if sel:
-                merge(i - 1)
+            trn, fin = 0 <= i - 1 < NCH, 0 <= i - 2 < NCH
+            if trn:
+                relu(i - 1)
             if nxt:
                 x_empty(i + 1, "ss")
+                offsets(i + 1)
             if now:
-                for n in range(3):
-                    long_z(i, n)
-                if i == 0:
-                    row_sums(0)
-                if i + 2 < NCH:
-                    x_transposes(i + 2)
-                for n in range(3):
-                    relu(i, n)
-                long_z(i, 3)
-                short_z(i, 0)
+                short_bias(i, 0)
+                short_bias(i, 1)
                 short_z(i, 1)
-                if i == 0:
-                    sign(0)
-                for n in range(3, 6):
-                    relu(i, n)
-                masks(i)
-            if nxt:
-                x_abs(i + 1)
-                x_quantize(i + 1)
-            if fin:
-                last_matmul(i - 2, 0)
-                last_matmul(i - 2, 1)
-            if nxt:
-                row_sums(i + 1)
+                long_bias(i, 0)
+                long_z(i, 2)
             if fin:
                 add_and_store(i - 2, 0)
                 last_matmul(i - 2, 2)
+            if trn:
+                h_transposes(i - 1)
+                h_empty(i - 1)
+            if now:
+                long_bias(i, 1)
+                long_z(i, 3)
+            if fin:
                 add_and_store(i - 2, 1)
                 last_matmul(i - 2, 3)
-                add_and_store(i - 2, 2)
-                add_and_store(i - 2, 3)
+            if now:
+                short_bias(i, 2)
+                short_bias(i, 3)
+                long_bias(i, 2)
+            if i + 2 < NCH:
+                x_transposes(i + 2)
+                row_sums(i + 2)
             if i == 0:
-                prepare_wf(0)
-                prepare_wf(1)
-            if sel:
-                regroup(i - 1)
+                bf_row = spread_row(D, D, ps_y, "y", "bf_row")
+                wf_banks = [weight_transposes(wf_sb, q, ps_y, "y") for q in range(2)]
+                empty(wf_banks[0], weight_part(gf, 0), "s")
+                empty(wf_banks[1], weight_part(gf, 1), "s")
             if nxt:
-                sign(i + 1)
+                x_quantize(i + 1)
+                long_z(i + 1, 0)
+                short_z(i + 1, 0)
+            if fin:
+                add_and_store(i - 2, 2)
+            if now:
+                long_bias(i, 3)
+            if nxt:
+                long_z(i + 1, 1)
+            if fin:
+                add_and_store(i - 2, 3)
+            if i == 1:
+                wfq = weight_quantize(gf, U1, "wf")
+            if trn:
+                h_quantize(i - 1)
+                last_matmul(i - 1, 0)
+                last_matmul(i - 1, 1)
+            if now:
+                merge(i)

@@ -189,11 +189,6 @@ def tile_dynamiclayer_t_kernel(tc, x, W1, b1, W2, b2, Wf, bf, out):
             nc.vector.tensor_tensor(out=low, in0=low, in1=state[("h2", c)][:].rearrange("p (r u) -> p r u", r=R),
                                     op=ALU.max)
 
-        def relu(c):
-            for q in range(2):
-                part = state[("h1", c)][:, q * 2 * U1:(q + 1) * 2 * U1]
-                nc.scalar.activation(out=part, in_=part, func=ACT.Relu)
-
         def h_transposes(c):
             hv = state[("h1", c)][:].bitcast(F32)
             banks = []
@@ -205,9 +200,11 @@ def tile_dynamiclayer_t_kernel(tc, x, W1, b1, W2, b2, Wf, bf, out):
 
         def h_empty(c):
             hg = work.tile([P, CH * 4], BF16, tag="hg", align_bytes=64)
-            gv = hg[:].bitcast(F32).rearrange("p (r j u) -> p r j u", r=4, u=2)
+            gv = hg[:].rearrange("p (r j u e) -> p r j u e", r=4, u=2, e=2)
             for q in range(2):
-                empty(state[("ht", c)][q], gv[:, 2 * q:2 * q + 2], "s")
+                src = state[("ht", c)][q][:].bitcast(BF16).rearrange("p (r u j e) -> p r j u e", r=2, u=2, e=2)
+                for r in range(2):
+                    nc.scalar.activation(out=gv[:, 2 * q + r], in_=src[:, r], func=ACT.Relu)
             state[("hg", c)] = hg
 
         def h_quantize(c):
@@ -265,8 +262,6 @@ def tile_dynamiclayer_t_kernel(tc, x, W1, b1, W2, b2, Wf, bf, out):
         for i in range(NCH + 2):
             now, nxt = i < NCH, i + 1 < NCH
             trn, fin = 0 <= i - 1 < NCH, 0 <= i - 2 < NCH
-            if trn:
-                relu(i - 1)
             if nxt:
                 x_empty(i + 1, "ss")
                 offsets(i + 1)

@@ -18,6 +18,7 @@ FLOPS = 2 * B * D * (U1 + U2) + 2 * B * U1 * D
 CH = 512
 R = CH // P
 NCH = B // CH
+POOL_TILES = (0,)
 SUP = 1024
 NSUP = B // SUP
 ROWS = U1 + D + U2
@@ -229,7 +230,12 @@ def tile_dynamiclayer_t_kernel(tc, x, W1, b1, W2, b2, Wf, bf, out):
                 osb = opool.tile([P, R * D], F32, tag="osb")
                 state[("o", c)] = osb
             osb = state[("o", c)]
-            nc.vector.tensor_tensor(out=osb[:, r * D:(r + 1) * D], in0=state[("y", c, r)][:], in1=bf_row[:], op=ALU.add)
+            part = osb[:, r * D:(r + 1) * D]
+            if r in POOL_TILES:
+                nc.scalar.copy(out=part, in_=state[("y", c, r)][:])
+                nc.gpsimd.tensor_tensor(out=part, in0=part, in1=bf_row[:], op=ALU.add)
+            else:
+                nc.vector.tensor_tensor(out=part, in0=state[("y", c, r)][:], in1=bf_row[:], op=ALU.add)
             last = c == NCH - 1
             if last or r == R - 1:
                 lo = r * D if last else 0
@@ -262,6 +268,9 @@ def tile_dynamiclayer_t_kernel(tc, x, W1, b1, W2, b2, Wf, bf, out):
         for i in range(NCH + 2):
             now, nxt = i < NCH, i + 1 < NCH
             trn, fin = 0 <= i - 1 < NCH, 0 <= i - 2 < NCH
+            if fin:
+                add_and_store(i - 2, 0)
+                last_matmul(i - 2, 2)
             if nxt:
                 x_empty(i + 1, "ss")
                 offsets(i + 1)
@@ -271,9 +280,6 @@ def tile_dynamiclayer_t_kernel(tc, x, W1, b1, W2, b2, Wf, bf, out):
                 short_z(i, 1)
                 long_bias(i, 0)
                 long_z(i, 2)
-            if fin:
-                add_and_store(i - 2, 0)
-                last_matmul(i - 2, 2)
             if trn:
                 h_transposes(i - 1)
                 h_empty(i - 1)

@@ -94,36 +94,48 @@ def tile_dynamiclayer_t_kernel(tc, x, W1, b1, W2, b2, Wf, bf, out):
             gv = g[:].bitcast(F32).rearrange("p (a j u) -> p a j u", j=P, u=2)
             return gv[:, 2 * q:2 * q + 2]
 
+        def empty_by_pairs(bank, g, q, engines):
+            gv = g[:].bitcast(F32).rearrange("p (v m e u) -> p v m e u", v=2, e=2, u=2)
+            bv = bank[:].rearrange("p (r u m v e) -> p r v m e u", r=2, u=2, v=2, e=2)
+            for r in range(2):
+                lo = (2 * q + r) * (P // 4)
+                for v in range(2):
+                    if engines[r] == "s":
+                        nc.scalar.copy(out=gv[:, v, lo:lo + P // 4], in_=bv[:, r, v])
+                    else:
+                        nc.vector.tensor_copy(out=gv[:, v, lo:lo + P // 4], in_=bv[:, r, v])
+
         def weight_quantize(g, units, name):
             codes = const.tile([P, units], U32, align_bytes=64, name="c_" + name)
             scales = const.tile([P, units], U8, align_bytes=64, name="s_" + name)
             nc.vector.quantize_mx(out=codes[:].bitcast(FP8X4), scales=scales[:], in_=g[:])
             return codes[:].bitcast(FP8X4), scales[:]
 
-        def spread_row(lo, width, pool, tag, name):
+        def spread_row(lo, width, pool, tag, name, by_pairs):
             bank = pool.tile([P, 512], F32, tag=tag, name="bank")
             nc.tensor.matmul(out=bank[:, 0:width], lhsT=ones[:], rhs=rows[:, lo:lo + width], start=True, stop=True)
             row = const.tile([P, width], BF16, name=name)
-            nc.scalar.copy(out=row[:], in_=bank[:, 0:width])
+            if by_pairs:
+                nc.scalar.copy(out=row[:].rearrange("p (v m e) -> p v m e", v=2, e=2),
+                               in_=bank[:, 0:width].rearrange("p (m v e) -> p v m e", v=2, e=2))
+            else:
+                nc.scalar.copy(out=row[:], in_=bank[:, 0:width])
             return row
 
         state = {}
 
-        def x_transposes(c):
+        def x_transposes(c, q):
             s, h = c // 2, c % 2
             xv = xs[s][:, h * 4 * D:(h + 1) * 4 * D].bitcast(F32)
-            banks = []
-            for q in range(2):
-                bank = ps_t.tile([P, 512], F32, tag="t", name="bank")
-                transposes(bank, words(xv, 2 * q) + words(xv, 2 * q + 1))
-                banks.append(bank)
-            state[("t", c)] = banks
+            bank = ps_t.tile([P, 512], F32, tag="t", name="bank")
+            transposes(bank, words(xv, 2 * q) + words(xv, 2 * q + 1))
+            state[("t", c, q)] = bank
 
         def x_empty(c, engines):
             xg = work.tile([P, CH * 4], BF16, tag="xg", align_bytes=64)
             gv = xg[:].bitcast(F32).rearrange("p (r j u) -> p r j u", r=4, u=2)
             for q in range(2):
-                empty(state[("t", c)][q], gv[:, 2 * q:2 * q + 2], engines[q])
+                empty(state[("t", c, q)], gv[:, 2 * q:2 * q + 2], engines[q])
             state[("g", c)] = xg
 
         def x_quantize(c):
@@ -186,24 +198,21 @@ def tile_dynamiclayer_t_kernel(tc, x, W1, b1, W2, b2, Wf, bf, out):
                                            op0=ALU.add, op1=ALU.add)
 
         def merge(c):
-            low = state[("h1", c)][:].rearrange("p (r u) -> p r u", r=R)[:, :, 0:U2]
-            nc.vector.tensor_tensor(out=low, in0=low, in1=state[("h2", c)][:].rearrange("p (r u) -> p r u", r=R),
+            low = state[("h1", c)][:].rearrange("p (g n) -> p g n", g=2 * R)[:, :, 0:U2 // 2]
+            nc.vector.tensor_tensor(out=low, in0=low, in1=state[("h2", c)][:].rearrange("p (g n) -> p g n", g=2 * R),
                                     op=ALU.max)
 
-        def h_transposes(c):
+        def h_transposes(c, q):
             hv = state[("h1", c)][:].bitcast(F32)
-            banks = []
-            for q in range(2):
-                bank = ps_t.tile([P, 512], F32, tag="t", name="bank")
-                transposes(bank, words(hv, 2 * q) + words(hv, 2 * q + 1))
-                banks.append(bank)
-            state[("ht", c)] = banks
+            bank = ps_t.tile([P, 512], F32, tag="t", name="bank")
+            transposes(bank, [hv[:, (4 * q + n) * P:(4 * q + n + 1) * P] for n in range(4)])
+            state[("ht", c, q)] = bank
 
         def h_empty(c):
             hg = work.tile([P, CH * 4], BF16, tag="hg", align_bytes=64)
             gv = hg[:].rearrange("p (r j u e) -> p r j u e", r=4, u=2, e=2)
             for q in range(2):
-                src = state[("ht", c)][q][:].bitcast(BF16).rearrange("p (r u j e) -> p r j u e", r=2, u=2, e=2)
+                src = state[("ht", c, q)][:].bitcast(BF16).rearrange("p (r u j e) -> p r j u e", r=2, u=2, e=2)
                 for r in range(2):
                     nc.scalar.activation(out=gv[:, 2 * q + r], in_=src[:, r], func=ACT.Relu)
             state[("hg", c)] = hg
@@ -246,20 +255,22 @@ def tile_dynamiclayer_t_kernel(tc, x, W1, b1, W2, b2, Wf, bf, out):
         g2 = weight_tile(U2, "w2")
         gf = weight_tile(U1, "wf")
         w1_banks = [weight_transposes(w1_sb, q, ps_z, "z") for q in range(2)]
-        empty(w1_banks[0], weight_part(g1, 0), "s")
-        empty(w1_banks[1], weight_part(g1, 1), "v")
-        x_transposes(0)
+        empty_by_pairs(w1_banks[0], g1, 0, "ss")
+        empty_by_pairs(w1_banks[1], g1, 1, "vv")
+        x_transposes(0, 0)
+        x_transposes(0, 1)
         w1q = weight_quantize(g1, U1, "w1")
         x_empty(0, "sv")
         w2_bank = weight_transposes(w2_sb, 0, ps_s, "s")
         row_sums(0)
         offsets(0)
         x_quantize(0)
-        empty(w2_bank, weight_part(g2, 0), "v")
+        empty_by_pairs(w2_bank, g2, 0, "vv")
         w2q = weight_quantize(g2, U2, "w2")
-        b2_row = spread_row(2 * D, U2, ps_y, "y", "b2_row")
-        b1_row = spread_row(0, U1, ps_y, "y", "b1_row")
-        x_transposes(1)
+        b2_row = spread_row(2 * D, U2, ps_y, "y", "b2_row", True)
+        b1_row = spread_row(0, U1, ps_y, "y", "b1_row", True)
+        x_transposes(1, 0)
+        x_transposes(1, 1)
         row_sums(1)
         long_z(0, 0)
         short_z(0, 0)
@@ -268,43 +279,50 @@ def tile_dynamiclayer_t_kernel(tc, x, W1, b1, W2, b2, Wf, bf, out):
         for i in range(NCH + 2):
             now, nxt = i < NCH, i + 1 < NCH
             trn, fin = 0 <= i - 1 < NCH, 0 <= i - 2 < NCH
+            enter = i + 2 < NCH
             if fin:
                 add_and_store(i - 2, 0)
-                last_matmul(i - 2, 2)
             if nxt:
                 x_empty(i + 1, "ss")
                 offsets(i + 1)
+            if trn:
+                h_transposes(i - 1, 0)
             if now:
                 short_bias(i, 0)
                 short_bias(i, 1)
                 short_z(i, 1)
+            if trn:
+                h_transposes(i - 1, 1)
+                h_empty(i - 1)
+            if now:
                 long_bias(i, 0)
                 long_z(i, 2)
-            if trn:
-                h_transposes(i - 1)
-                h_empty(i - 1)
+            if fin:
+                last_matmul(i - 2, 2)
             if now:
                 long_bias(i, 1)
                 long_z(i, 3)
+            if enter:
+                x_transposes(i + 2, 0)
             if fin:
                 add_and_store(i - 2, 1)
                 last_matmul(i - 2, 3)
+            if enter:
+                x_transposes(i + 2, 1)
+                row_sums(i + 2)
             if now:
                 short_bias(i, 2)
                 short_bias(i, 3)
                 long_bias(i, 2)
-            if i + 2 < NCH:
-                x_transposes(i + 2)
-                row_sums(i + 2)
             if i == 0:
-                bf_row = spread_row(D, D, ps_y, "y", "bf_row")
+                bf_row = spread_row(D, D, ps_y, "y", "bf_row", False)
                 wf_banks = [weight_transposes(wf_sb, q, ps_y, "y") for q in range(2)]
                 empty(wf_banks[0], weight_part(gf, 0), "s")
                 empty(wf_banks[1], weight_part(gf, 1), "s")
             if nxt:
                 x_quantize(i + 1)
-                long_z(i + 1, 0)
                 short_z(i + 1, 0)
+                long_z(i + 1, 0)
             if fin:
                 add_and_store(i - 2, 2)
             if now:

@@ -208,26 +208,36 @@ def tile_dynamiclayer_t_kernel(tc, x, W1, b1, W2, b2, Wf, bf, out):
             transposes(bank, [hv[:, (4 * q + n) * P:(4 * q + n + 1) * P] for n in range(4)])
             state[("ht", c, q)] = bank
 
-        def h_empty(c):
-            hg = work.tile([P, CH * 4], BF16, tag="hg", align_bytes=64)
-            gv = hg[:].rearrange("p (r j u e) -> p r j u e", r=4, u=2, e=2)
-            for q in range(2):
-                src = state[("ht", c, q)][:].bitcast(BF16).rearrange("p (r u j e) -> p r j u e", r=2, u=2, e=2)
-                for r in range(2):
+        def h_empty(c, q, engine):
+            if ("hg", c) not in state:
+                hg = work.tile([P, CH * 4], BF16, tag="hg", align_bytes=64)
+                state[("hg", c)] = hg
+            gv = state[("hg", c)][:].rearrange("p (r j u e) -> p r j u e", r=4, u=2, e=2)
+            src = state[("ht", c, q)][:].bitcast(BF16).rearrange("p (r u j e) -> p r j u e", r=2, u=2, e=2)
+            for r in range(2):
+                if engine == "s":
                     nc.scalar.activation(out=gv[:, 2 * q + r], in_=src[:, r], func=ACT.Relu)
-            state[("hg", c)] = hg
+                else:
+                    nc.vector.tensor_scalar(out=gv[:, 2 * q + r], in0=src[:, r], scalar1=0.0, scalar2=None, op0=ALU.max)
 
-        def h_quantize(c):
-            hc = work.tile([P, CH], U32, tag="hc", align_bytes=64)
-            hs = work.tile([P, CH], U8, tag="hs", align_bytes=64)
-            nc.vector.quantize_mx(out=hc[:].bitcast(FP8X4), scales=hs[:], in_=state[("hg", c)][:])
-            state[("h", c)] = (hc, hs)
+        def h_quantize(c, tiles):
+            if ("h", c) not in state:
+                hc = work.tile([P, CH], U32, tag="hc", align_bytes=64)
+                hs = work.tile([P, CH], U8, tag="hs", align_bytes=64)
+                state[("h", c)] = (hc, hs)
+            hc, hs = state[("h", c)]
+            cols = slice(tiles[0] * P, (tiles[-1] + 1) * P)
+            nc.vector.quantize_mx(out=hc[:, cols].bitcast(FP8X4), scales=hs[:, cols],
+                                  in_=state[("hg", c)][:, cols.start * 4:cols.stop * 4])
 
         out_view = out.rearrange("(s p r) d -> s p (r d)", p=P, r=SUP // P)
 
         def last_matmul(c, r):
             hc, hs = state[("h", c)]
-            y = ps_y.tile([P, D], F32, tag="y")
+            if c == NCH - 1 and r > 1:
+                y = ps_z.tile([P, D], F32, tag="z")
+            else:
+                y = ps_y.tile([P, D], F32, tag="y")
             nc.tensor.matmul_mx(out=y[:], lhsT=hc[:, r * P:(r + 1) * P].bitcast(FP8X4),
                                 lhsT_scale=hs[:, r * P:(r + 1) * P],
                                 rhs=wfq[0], rhs_scale=wfq[1], start=True, stop=True)
@@ -235,7 +245,7 @@ def tile_dynamiclayer_t_kernel(tc, x, W1, b1, W2, b2, Wf, bf, out):
 
         def add_and_store(c, r):
             s, h = c // 2, c % 2
-            if r == 0:
+            if ("o", c) not in state:
                 osb = opool.tile([P, R * D], F32, tag="osb")
                 state[("o", c)] = osb
             osb = state[("o", c)]
@@ -245,23 +255,38 @@ def tile_dynamiclayer_t_kernel(tc, x, W1, b1, W2, b2, Wf, bf, out):
                 nc.gpsimd.tensor_tensor(out=part, in0=part, in1=bf_row[:], op=ALU.add)
             else:
                 nc.vector.tensor_tensor(out=part, in0=state[("y", c, r)][:], in1=bf_row[:], op=ALU.add)
-            last = c == NCH - 1
+            last = c >= NCH - 2
             if last or r == R - 1:
                 lo = r * D if last else 0
                 nc.sync.dma_start(out=out_view[s][:, h * R * D + lo:h * R * D + (r + 1) * D],
                                   in_=osb[:, lo:(r + 1) * D])
 
+        filler = const.tile([P, D], BF16)
+        nc.vector.memset(filler[:], 0.0)
+
+        def keep_warm(n):
+            for e in range(n):
+                bank = ps_y.tile([P, D], F32, tag="y", name="bank")
+                nc.tensor.matmul(out=bank[:], lhsT=ones[:], rhs=filler[:], start=True, stop=True)
+
         g1 = weight_tile(U1, "w1")
         g2 = weight_tile(U2, "w2")
         gf = weight_tile(U1, "wf")
-        w1_banks = [weight_transposes(w1_sb, q, ps_z, "z") for q in range(2)]
+        keep_warm(6)
+        w1_banks = []
+        for q in range(2):
+            w1_banks.append(weight_transposes(w1_sb, q, ps_z, "z"))
+            keep_warm(1)
         empty_by_pairs(w1_banks[0], g1, 0, "ss")
         empty_by_pairs(w1_banks[1], g1, 1, "vv")
         x_transposes(0, 0)
+        keep_warm(1)
         x_transposes(0, 1)
+        keep_warm(1)
         w1q = weight_quantize(g1, U1, "w1")
         x_empty(0, "sv")
         w2_bank = weight_transposes(w2_sb, 0, ps_s, "s")
+        keep_warm(1)
         row_sums(0)
         offsets(0)
         x_quantize(0)
@@ -269,16 +294,16 @@ def tile_dynamiclayer_t_kernel(tc, x, W1, b1, W2, b2, Wf, bf, out):
         w2q = weight_quantize(g2, U2, "w2")
         b2_row = spread_row(2 * D, U2, ps_y, "y", "b2_row", True)
         b1_row = spread_row(0, U1, ps_y, "y", "b1_row", True)
+        short_z(0, 0)
+        long_z(0, 0)
+        long_z(0, 1)
         x_transposes(1, 0)
         x_transposes(1, 1)
         row_sums(1)
-        long_z(0, 0)
-        short_z(0, 0)
-        long_z(0, 1)
 
-        for i in range(NCH + 2):
-            now, nxt = i < NCH, i + 1 < NCH
-            trn, fin = 0 <= i - 1 < NCH, 0 <= i - 2 < NCH
+        for i in range(NCH):
+            now, nxt = True, i + 1 < NCH
+            trn, fin = i >= 1, i >= 2
             enter = i + 2 < NCH
             if fin:
                 add_and_store(i - 2, 0)
@@ -293,7 +318,8 @@ def tile_dynamiclayer_t_kernel(tc, x, W1, b1, W2, b2, Wf, bf, out):
                 short_z(i, 1)
             if trn:
                 h_transposes(i - 1, 1)
-                h_empty(i - 1)
+                h_empty(i - 1, 0, "s")
+                h_empty(i - 1, 1, "s")
             if now:
                 long_bias(i, 0)
                 long_z(i, 2)
@@ -302,6 +328,10 @@ def tile_dynamiclayer_t_kernel(tc, x, W1, b1, W2, b2, Wf, bf, out):
             if now:
                 long_bias(i, 1)
                 long_z(i, 3)
+            if i == 1:
+                for q in range(2):
+                    empty(weight_transposes(wf_sb, q, ps_y, "y"), weight_part(gf, q), "s")
+                bf_row = spread_row(D, D, ps_y, "y", "bf_row", False)
             if enter:
                 x_transposes(i + 2, 0)
             if fin:
@@ -314,11 +344,6 @@ def tile_dynamiclayer_t_kernel(tc, x, W1, b1, W2, b2, Wf, bf, out):
                 short_bias(i, 2)
                 short_bias(i, 3)
                 long_bias(i, 2)
-            if i == 0:
-                bf_row = spread_row(D, D, ps_y, "y", "bf_row", False)
-                wf_banks = [weight_transposes(wf_sb, q, ps_y, "y") for q in range(2)]
-                empty(wf_banks[0], weight_part(gf, 0), "s")
-                empty(wf_banks[1], weight_part(gf, 1), "s")
             if nxt:
                 x_quantize(i + 1)
                 short_z(i + 1, 0)
@@ -334,8 +359,28 @@ def tile_dynamiclayer_t_kernel(tc, x, W1, b1, W2, b2, Wf, bf, out):
             if i == 1:
                 wfq = weight_quantize(gf, U1, "wf")
             if trn:
-                h_quantize(i - 1)
+                h_quantize(i - 1, (0, 1, 2, 3))
                 last_matmul(i - 1, 0)
                 last_matmul(i - 1, 1)
             if now:
                 merge(i)
+
+        c = NCH - 1
+        h_transposes(c, 0)
+        add_and_store(c - 1, 0)
+        h_transposes(c, 1)
+        h_empty(c, 0, "s")
+        add_and_store(c - 1, 1)
+        h_empty(c, 1, "v")
+        last_matmul(c - 1, 2)
+        last_matmul(c - 1, 3)
+        h_quantize(c, (0, 1))
+        h_quantize(c, (2, 3))
+        add_and_store(c - 1, 2)
+        last_matmul(c, 0)
+        add_and_store(c - 1, 3)
+        last_matmul(c, 1)
+        last_matmul(c, 2)
+        last_matmul(c, 3)
+        for r in (1, 0, 2, 3):
+            add_and_store(c, r)

@@ -18,7 +18,7 @@ FLOPS = 2 * B * D * (U1 + U2) + 2 * B * U1 * D
 CH = 512
 R = CH // P
 NCH = B // CH
-POOL_TILES = (0,)
+POOL_TILES = (0, 2)
 SUP = 1024
 NSUP = B // SUP
 ROWS = U1 + D + U2
@@ -250,7 +250,7 @@ def tile_dynamiclayer_t_kernel(tc, x, W1, b1, W2, b2, Wf, bf, out):
                 state[("o", c)] = osb
             osb = state[("o", c)]
             part = osb[:, r * D:(r + 1) * D]
-            if r in POOL_TILES:
+            if r in POOL_TILES and c < NCH - 2 or r == 0:
                 nc.scalar.copy(out=part, in_=state[("y", c, r)][:])
                 nc.gpsimd.tensor_tensor(out=part, in0=part, in1=bf_row[:], op=ALU.add)
             else:
@@ -337,6 +337,7 @@ def tile_dynamiclayer_t_kernel(tc, x, W1, b1, W2, b2, Wf, bf, out):
             if fin:
                 add_and_store(i - 2, 1)
                 last_matmul(i - 2, 3)
+                add_and_store(i - 2, 2)
             if enter:
                 x_transposes(i + 2, 1)
                 row_sums(i + 2)
@@ -348,19 +349,18 @@ def tile_dynamiclayer_t_kernel(tc, x, W1, b1, W2, b2, Wf, bf, out):
                 x_quantize(i + 1)
                 short_z(i + 1, 0)
                 long_z(i + 1, 0)
-            if fin:
-                add_and_store(i - 2, 2)
+            if i == 1:
+                wfq = weight_quantize(gf, U1, "wf")
+            if trn:
+                h_quantize(i - 1, (0, 1, 2, 3))
+                last_matmul(i - 1, 0)
             if now:
                 long_bias(i, 3)
             if nxt:
                 long_z(i + 1, 1)
             if fin:
                 add_and_store(i - 2, 3)
-            if i == 1:
-                wfq = weight_quantize(gf, U1, "wf")
             if trn:
-                h_quantize(i - 1, (0, 1, 2, 3))
-                last_matmul(i - 1, 0)
                 last_matmul(i - 1, 1)
             if now:
                 merge(i)

@@ -54,8 +54,11 @@ def tile_dynamiclayer_t_kernel(tc, x, W1, b1, W2, b2, Wf, bf, out):
         for s in range(NSUP):
             xt_sb = xpool.tile([P, (SUP // P) * D], BF16, name="x%d" % s)
             xs.append(xt_sb)
-        nc.sync.dma_start(out=w1_sb[:], in_=W1.rearrange("(a p) k -> p a k", p=P))
-        nc.sync.dma_start(out=xs[0][:, 0:4 * D], in_=x_view[0][:, 0:4 * D])
+        w1_view = W1.rearrange("(a p) k -> p a k", p=P)
+        for q in range(2):
+            nc.sync.dma_start(out=xs[0][:, q * 2 * D:(q + 1) * 2 * D], in_=x_view[0][:, q * 2 * D:(q + 1) * 2 * D])
+        for q in range(2):
+            nc.sync.dma_start(out=w1_sb[:, 2 * q:2 * q + 2], in_=w1_view[:, 2 * q:2 * q + 2])
         nc.sync.dma_start(out=w2_sb[:], in_=W2.rearrange("(a p) k -> p a k", p=P))
         nc.sync.dma_start(out=xs[0][:, 4 * D:8 * D], in_=x_view[0][:, 4 * D:8 * D])
         nc.sync.dma_start(out=wf_sb[:], in_=Wf.rearrange("(a p) u -> p a u", p=P))
@@ -131,12 +134,13 @@ def tile_dynamiclayer_t_kernel(tc, x, W1, b1, W2, b2, Wf, bf, out):
             transposes(bank, words(xv, 2 * q) + words(xv, 2 * q + 1))
             state[("t", c, q)] = bank
 
-        def x_empty(c, engines):
-            xg = work.tile([P, CH * 4], BF16, tag="xg", align_bytes=64)
-            gv = xg[:].bitcast(F32).rearrange("p (r j u) -> p r j u", r=4, u=2)
-            for q in range(2):
+        def x_empty(c, engines, banks=(0, 1)):
+            if ("g", c) not in state:
+                xg = work.tile([P, CH * 4], BF16, tag="xg", align_bytes=64)
+                state[("g", c)] = xg
+            gv = state[("g", c)][:].bitcast(F32).rearrange("p (r j u) -> p r j u", r=4, u=2)
+            for q in banks:
                 empty(state[("t", c, q)], gv[:, 2 * q:2 * q + 2], engines[q])
-            state[("g", c)] = xg
 
         def x_quantize(c):
             xc = work.tile([P, CH], U32, tag="xc", align_bytes=64)
@@ -234,7 +238,7 @@ def tile_dynamiclayer_t_kernel(tc, x, W1, b1, W2, b2, Wf, bf, out):
 
         def last_matmul(c, r):
             hc, hs = state[("h", c)]
-            if c == NCH - 1 and r > 1:
+            if c == NCH - 1 and r < 2:
                 y = ps_z.tile([P, D], F32, tag="z")
             else:
                 y = ps_y.tile([P, D], F32, tag="y")
@@ -273,24 +277,23 @@ def tile_dynamiclayer_t_kernel(tc, x, W1, b1, W2, b2, Wf, bf, out):
         g2 = weight_tile(U2, "w2")
         gf = weight_tile(U1, "wf")
         keep_warm(6)
+        for q in range(2):
+            x_transposes(0, q)
+            keep_warm(1)
+        row_sums(0)
+        offsets(0)
+        x_empty(0, "vv")
         w1_banks = []
         for q in range(2):
             w1_banks.append(weight_transposes(w1_sb, q, ps_z, "z"))
             keep_warm(1)
-        empty_by_pairs(w1_banks[0], g1, 0, "ss")
-        empty_by_pairs(w1_banks[1], g1, 1, "vv")
-        x_transposes(0, 0)
-        keep_warm(1)
-        x_transposes(0, 1)
-        keep_warm(1)
-        w1q = weight_quantize(g1, U1, "w1")
-        x_empty(0, "sv")
         w2_bank = weight_transposes(w2_sb, 0, ps_s, "s")
         keep_warm(1)
-        row_sums(0)
-        offsets(0)
         x_quantize(0)
-        empty_by_pairs(w2_bank, g2, 0, "vv")
+        empty_by_pairs(w1_banks[0], g1, 0, "ss")
+        empty_by_pairs(w1_banks[1], g1, 1, "vv")
+        empty_by_pairs(w2_bank, g2, 0, "ss")
+        w1q = weight_quantize(g1, U1, "w1")
         w2q = weight_quantize(g2, U2, "w2")
         b2_row = spread_row(2 * D, U2, ps_y, "y", "b2_row", True)
         b1_row = spread_row(0, U1, ps_y, "y", "b1_row", True)
@@ -305,10 +308,12 @@ def tile_dynamiclayer_t_kernel(tc, x, W1, b1, W2, b2, Wf, bf, out):
             now, nxt = True, i + 1 < NCH
             trn, fin = i >= 1, i >= 2
             enter = i + 2 < NCH
+            if nxt:
+                x_empty(i + 1, "ss", (0,))
             if fin:
                 add_and_store(i - 2, 0)
             if nxt:
-                x_empty(i + 1, "ss")
+                x_empty(i + 1, "ss", (1,))
                 offsets(i + 1)
             if trn:
                 h_transposes(i - 1, 0)
@@ -328,17 +333,16 @@ def tile_dynamiclayer_t_kernel(tc, x, W1, b1, W2, b2, Wf, bf, out):
             if now:
                 long_bias(i, 1)
                 long_z(i, 3)
+            if i == 0:
+                wf_banks = [weight_transposes(wf_sb, q, ps_y, "y") for q in range(2)]
             if i == 1:
-                for q in range(2):
-                    empty(weight_transposes(wf_sb, q, ps_y, "y"), weight_part(gf, q), "s")
                 bf_row = spread_row(D, D, ps_y, "y", "bf_row", False)
-            if enter:
-                x_transposes(i + 2, 0)
             if fin:
                 add_and_store(i - 2, 1)
                 last_matmul(i - 2, 3)
                 add_and_store(i - 2, 2)
             if enter:
+                x_transposes(i + 2, 0)
                 x_transposes(i + 2, 1)
                 row_sums(i + 2)
             if now:
@@ -349,8 +353,6 @@ def tile_dynamiclayer_t_kernel(tc, x, W1, b1, W2, b2, Wf, bf, out):
                 x_quantize(i + 1)
                 short_z(i + 1, 0)
                 long_z(i + 1, 0)
-            if i == 1:
-                wfq = weight_quantize(gf, U1, "wf")
             if trn:
                 h_quantize(i - 1, (0, 1, 2, 3))
                 last_matmul(i - 1, 0)
@@ -364,6 +366,10 @@ def tile_dynamiclayer_t_kernel(tc, x, W1, b1, W2, b2, Wf, bf, out):
                 last_matmul(i - 1, 1)
             if now:
                 merge(i)
+            if i == 0:
+                for q in range(2):
+                    empty(wf_banks[q], weight_part(gf, q), "v")
+                wfq = weight_quantize(gf, U1, "wf")
 
         c = NCH - 1
         h_transposes(c, 0)

@@ -148,11 +148,13 @@ def tile_dynamiclayer_t_kernel(tc, x, W1, b1, W2, b2, Wf, bf, out):
             nc.vector.quantize_mx(out=xc[:].bitcast(FP8X4), scales=xsc[:], in_=state[("g", c)][:])
             state[("x", c)] = (xc, xsc)
 
-        def row_sums(c):
+        def row_sums(c, tiles):
             s, h = c // 2, c % 2
-            ssum = work.tile([P, R], F32, tag="ssum")
-            state[("s", c)] = ssum
-            for r in range(R):
+            if ("s", c) not in state:
+                ssum = work.tile([P, R], F32, tag="ssum")
+                state[("s", c)] = ssum
+            ssum = state[("s", c)]
+            for r in tiles:
                 junk = work.tile([P, D], BF16, tag="junk")
                 lo = (h * R + r) * D
                 nc.scalar.activation(out=junk[:], in_=xs[s][:, lo:lo + D], func=ACT.Abs, accum_out=ssum[:, r:r + 1])
@@ -212,13 +214,13 @@ def tile_dynamiclayer_t_kernel(tc, x, W1, b1, W2, b2, Wf, bf, out):
             transposes(bank, [hv[:, (4 * q + n) * P:(4 * q + n + 1) * P] for n in range(4)])
             state[("ht", c, q)] = bank
 
-        def h_empty(c, q, engine):
+        def h_empty(c, q, engine, tiles=(0, 1)):
             if ("hg", c) not in state:
                 hg = work.tile([P, CH * 4], BF16, tag="hg", align_bytes=64)
                 state[("hg", c)] = hg
             gv = state[("hg", c)][:].rearrange("p (r j u e) -> p r j u e", r=4, u=2, e=2)
             src = state[("ht", c, q)][:].bitcast(BF16).rearrange("p (r u j e) -> p r j u e", r=2, u=2, e=2)
-            for r in range(2):
+            for r in tiles:
                 if engine == "s":
                     nc.scalar.activation(out=gv[:, 2 * q + r], in_=src[:, r], func=ACT.Relu)
                 else:
@@ -280,7 +282,7 @@ def tile_dynamiclayer_t_kernel(tc, x, W1, b1, W2, b2, Wf, bf, out):
         for q in range(2):
             x_transposes(0, q)
             keep_warm(1)
-        row_sums(0)
+        row_sums(0, range(R))
         offsets(0)
         x_empty(0, "vv")
         w1_banks = []
@@ -302,7 +304,7 @@ def tile_dynamiclayer_t_kernel(tc, x, W1, b1, W2, b2, Wf, bf, out):
         long_z(0, 1)
         x_transposes(1, 0)
         x_transposes(1, 1)
-        row_sums(1)
+        row_sums(1, range(R))
 
         for i in range(NCH):
             now, nxt = True, i + 1 < NCH
@@ -324,7 +326,7 @@ def tile_dynamiclayer_t_kernel(tc, x, W1, b1, W2, b2, Wf, bf, out):
             if trn:
                 h_transposes(i - 1, 1)
                 h_empty(i - 1, 0, "s")
-                h_empty(i - 1, 1, "s")
+                h_empty(i - 1, 1, "s", (0,))
             if now:
                 long_bias(i, 0)
                 long_z(i, 2)
@@ -340,11 +342,12 @@ def tile_dynamiclayer_t_kernel(tc, x, W1, b1, W2, b2, Wf, bf, out):
             if fin:
                 add_and_store(i - 2, 1)
                 last_matmul(i - 2, 3)
+            if fin:
                 add_and_store(i - 2, 2)
             if enter:
                 x_transposes(i + 2, 0)
                 x_transposes(i + 2, 1)
-                row_sums(i + 2)
+                row_sums(i + 2, range(R))
             if now:
                 short_bias(i, 2)
                 short_bias(i, 3)
@@ -354,8 +357,7 @@ def tile_dynamiclayer_t_kernel(tc, x, W1, b1, W2, b2, Wf, bf, out):
                 short_z(i + 1, 0)
                 long_z(i + 1, 0)
             if trn:
-                h_quantize(i - 1, (0, 1, 2, 3))
-                last_matmul(i - 1, 0)
+                h_empty(i - 1, 1, "v", (1,))
             if now:
                 long_bias(i, 3)
             if nxt:
@@ -363,6 +365,8 @@ def tile_dynamiclayer_t_kernel(tc, x, W1, b1, W2, b2, Wf, bf, out):
             if fin:
                 add_and_store(i - 2, 3)
             if trn:
+                h_quantize(i - 1, (0, 1, 2, 3))
+                last_matmul(i - 1, 0)
                 last_matmul(i - 1, 1)
             if now:
                 merge(i)

@@ -18,11 +18,15 @@ FLOPS = 2 * B * D * (U1 + U2) + 2 * B * U1 * D
 CH = 512
 R = CH // P
 NCH = B // CH
-POOL_TILES = (0, 2)
+POOL_TILES = (0, 1, 2)
 SUP = 1024
 NSUP = B // SUP
 ROWS = U1 + D + U2
 OFF = -3.0e38
+
+
+def pool_tiles(c):
+    return POOL_TILES if c < NCH - 3 else (0,)
 
 
 def tile_dynamiclayer_t_kernel(tc, x, W1, b1, W2, b2, Wf, bf, out):
@@ -126,6 +130,7 @@ def tile_dynamiclayer_t_kernel(tc, x, W1, b1, W2, b2, Wf, bf, out):
             return row
 
         state = {}
+        TAGS = {ps_y: "y", ps_z: "z", ps_s: "s"}
 
         def x_transposes(c, q):
             s, h = c // 2, c % 2
@@ -203,9 +208,11 @@ def tile_dynamiclayer_t_kernel(tc, x, W1, b1, W2, b2, Wf, bf, out):
                                            scalar=state[("off", c)][1][:, r:r + 1], in1=b2_row[:],
                                            op0=ALU.add, op1=ALU.add)
 
-        def merge(c):
-            low = state[("h1", c)][:].rearrange("p (g n) -> p g n", g=2 * R)[:, :, 0:U2 // 2]
-            nc.vector.tensor_tensor(out=low, in0=low, in1=state[("h2", c)][:].rearrange("p (g n) -> p g n", g=2 * R),
+        def merge(c, tiles=(0, R)):
+            runs = slice(2 * tiles[0], 2 * tiles[1])
+            low = state[("h1", c)][:].rearrange("p (g n) -> p g n", g=2 * R)[:, runs, 0:U2 // 2]
+            nc.vector.tensor_tensor(out=low, in0=low,
+                                    in1=state[("h2", c)][:].rearrange("p (g n) -> p g n", g=2 * R)[:, runs],
                                     op=ALU.max)
 
         def h_transposes(c, q):
@@ -238,34 +245,30 @@ def tile_dynamiclayer_t_kernel(tc, x, W1, b1, W2, b2, Wf, bf, out):
 
         out_view = out.rearrange("(s p r) d -> s p (r d)", p=P, r=SUP // P)
 
-        def last_matmul(c, r):
+        def last_matmul(c, r, pool=ps_y):
             hc, hs = state[("h", c)]
-            if c == NCH - 1 and r < 2:
-                y = ps_z.tile([P, D], F32, tag="z")
-            else:
-                y = ps_y.tile([P, D], F32, tag="y")
+            y = pool.tile([P, D], F32, tag=TAGS[pool], name="y")
             nc.tensor.matmul_mx(out=y[:], lhsT=hc[:, r * P:(r + 1) * P].bitcast(FP8X4),
                                 lhsT_scale=hs[:, r * P:(r + 1) * P],
                                 rhs=wfq[0], rhs_scale=wfq[1], start=True, stop=True)
             state[("y", c, r)] = y
 
-        def add_and_store(c, r):
-            s, h = c // 2, c % 2
+        def add_bias(c, r):
             if ("o", c) not in state:
                 osb = opool.tile([P, R * D], F32, tag="osb")
                 state[("o", c)] = osb
             osb = state[("o", c)]
             part = osb[:, r * D:(r + 1) * D]
-            if r in POOL_TILES and c < NCH - 2 or r == 0:
+            if r in pool_tiles(c):
                 nc.scalar.copy(out=part, in_=state[("y", c, r)][:])
                 nc.gpsimd.tensor_tensor(out=part, in0=part, in1=bf_row[:], op=ALU.add)
             else:
                 nc.vector.tensor_tensor(out=part, in0=state[("y", c, r)][:], in1=bf_row[:], op=ALU.add)
-            last = c >= NCH - 2
-            if last or r == R - 1:
-                lo = r * D if last else 0
-                nc.sync.dma_start(out=out_view[s][:, h * R * D + lo:h * R * D + (r + 1) * D],
-                                  in_=osb[:, lo:(r + 1) * D])
+
+        def store(c, tiles):
+            s, h = c // 2, c % 2
+            lo, hi = tiles[0] * D, (tiles[-1] + 1) * D
+            nc.sync.dma_start(out=out_view[s][:, h * R * D + lo:h * R * D + hi], in_=state[("o", c)][:, lo:hi])
 
         filler = const.tile([P, D], BF16)
         nc.vector.memset(filler[:], 0.0)
@@ -306,91 +309,117 @@ def tile_dynamiclayer_t_kernel(tc, x, W1, b1, W2, b2, Wf, bf, out):
         x_transposes(1, 1)
         row_sums(1, range(R))
 
-        for i in range(NCH):
-            now, nxt = True, i + 1 < NCH
+        for i in range(NCH - 1):
             trn, fin = i >= 1, i >= 2
             enter = i + 2 < NCH
-            if nxt:
-                x_empty(i + 1, "ss", (0,))
+            x_empty(i + 1, "ss", (0,))
             if fin:
-                add_and_store(i - 2, 0)
-            if nxt:
-                x_empty(i + 1, "ss", (1,))
-                offsets(i + 1)
+                add_bias(i - 2, 1)
+            x_empty(i + 1, "ss", (1,))
+            offsets(i + 1)
             if trn:
                 h_transposes(i - 1, 0)
-            if now:
-                short_bias(i, 0)
-                short_bias(i, 1)
-                short_z(i, 1)
+            short_bias(i, 0)
+            short_bias(i, 1)
+            short_z(i, 1)
             if trn:
                 h_transposes(i - 1, 1)
                 h_empty(i - 1, 0, "s")
-                h_empty(i - 1, 1, "s", (0,))
-            if now:
-                long_bias(i, 0)
-                long_z(i, 2)
+            long_bias(i, 0)
+            long_z(i, 2)
             if fin:
                 last_matmul(i - 2, 2)
-            if now:
-                long_bias(i, 1)
-                long_z(i, 3)
+            long_bias(i, 1)
+            long_z(i, 3)
             if i == 0:
                 wf_banks = [weight_transposes(wf_sb, q, ps_y, "y") for q in range(2)]
             if i == 1:
                 bf_row = spread_row(D, D, ps_y, "y", "bf_row", False)
             if fin:
-                add_and_store(i - 2, 1)
                 last_matmul(i - 2, 3)
-            if fin:
-                add_and_store(i - 2, 2)
             if enter:
                 x_transposes(i + 2, 0)
                 x_transposes(i + 2, 1)
-                row_sums(i + 2, range(R))
-            if now:
-                short_bias(i, 2)
-                short_bias(i, 3)
-                long_bias(i, 2)
-            if nxt:
-                x_quantize(i + 1)
-                short_z(i + 1, 0)
-                long_z(i + 1, 0)
+                row_sums(i + 2, range(2))
+            short_bias(i, 2)
+            short_bias(i, 3)
+            long_bias(i, 2)
             if trn:
-                h_empty(i - 1, 1, "v", (1,))
-            if now:
-                long_bias(i, 3)
-            if nxt:
-                long_z(i + 1, 1)
+                h_empty(i - 1, 1, "v" if enter else "s")
             if fin:
-                add_and_store(i - 2, 3)
+                add_bias(i - 2, 2)
+            if enter:
+                row_sums(i + 2, range(2, R))
+            x_quantize(i + 1)
+            short_z(i + 1, 0)
+            long_z(i + 1, 0)
+            if i == 1:
+                wfq = weight_quantize(gf, U1, "wf")
             if trn:
                 h_quantize(i - 1, (0, 1, 2, 3))
                 last_matmul(i - 1, 0)
+            long_bias(i, 3)
+            long_z(i + 1, 1)
+            if fin:
+                add_bias(i - 2, 3)
+                store(i - 2, range(R))
+            if trn:
                 last_matmul(i - 1, 1)
-            if now:
-                merge(i)
+                add_bias(i - 1, 0)
+            merge(i)
             if i == 0:
                 for q in range(2):
-                    empty(wf_banks[q], weight_part(gf, q), "v")
-                wfq = weight_quantize(gf, U1, "wf")
+                    empty(wf_banks[q], weight_part(gf, q), "ss"[q])
 
         c = NCH - 1
+        h_transposes(c - 1, 0)
+        short_bias(c, 0)
+        short_bias(c, 1)
+        short_z(c, 1)
+        h_transposes(c - 1, 1)
+        h_empty(c - 1, 0, "s")
+        h_empty(c - 1, 1, "s")
+        long_bias(c, 0)
+        long_z(c, 2)
+        last_matmul(c - 2, 2)
+        long_bias(c, 1)
+        long_z(c, 3)
+        add_bias(c - 2, 1)
+        store(c - 2, (0, 1))
+        last_matmul(c - 2, 3)
+        merge(c, (0, 2))
         h_transposes(c, 0)
-        add_and_store(c - 1, 0)
-        h_transposes(c, 1)
         h_empty(c, 0, "s")
-        add_and_store(c - 1, 1)
-        h_empty(c, 1, "v")
-        last_matmul(c - 1, 2)
+        short_bias(c, 2)
+        short_bias(c, 3)
+        h_quantize(c - 1, (0, 1, 2, 3))
+        last_matmul(c - 1, 0, ps_s)
+        long_bias(c, 2)
+        last_matmul(c - 1, 1, ps_z)
+        long_bias(c, 3)
+        last_matmul(c - 1, 2, ps_z)
+        add_bias(c - 1, 0)
+        add_bias(c - 2, 2)
         last_matmul(c - 1, 3)
+        add_bias(c - 2, 3)
+        store(c - 2, (2, 3))
+        add_bias(c - 1, 1)
+        store(c - 1, (0, 1))
+        merge(c, (2, R))
+        h_transposes(c, 1)
         h_quantize(c, (0, 1))
-        h_quantize(c, (2, 3))
-        add_and_store(c - 1, 2)
         last_matmul(c, 0)
-        add_and_store(c - 1, 3)
-        last_matmul(c, 1)
-        last_matmul(c, 2)
-        last_matmul(c, 3)
-        for r in (1, 0, 2, 3):
-            add_and_store(c, r)
+        last_matmul(c, 1, ps_s)
+        h_empty(c, 1, "s", (0,))
+        add_bias(c - 1, 2)
+        store(c - 1, (2,))
+        h_empty(c, 1, "v", (1,))
+        add_bias(c - 1, 3)
+        store(c - 1, (3,))
+        h_quantize(c, (2, 3))
+        last_matmul(c, 2, ps_z)
+        last_matmul(c, 3, ps_z)
+        for r in range(R):
+            add_bias(c, r)
+        for r in (1, 2, 0, 3):
+            store(c, (r,))

@@ -218,20 +218,21 @@ def tile_dynamiclayer_t_kernel(tc, x, W1, b1, W2, b2, Wf, bf, out):
         def h_transposes(c, q):
             hv = state[("h1", c)][:].bitcast(F32)
             bank = ps_t.tile([P, 512], F32, tag="t", name="bank")
-            transposes(bank, [hv[:, (4 * q + n) * P:(4 * q + n + 1) * P] for n in range(4)])
+            transposes(bank, [hv[:, (4 * q + 2 * r + u) * P:(4 * q + 2 * r + u + 1) * P] for u in range(2) for r in range(2)])
             state[("ht", c, q)] = bank
 
         def h_empty(c, q, engine, tiles=(0, 1)):
             if ("hg", c) not in state:
                 hg = work.tile([P, CH * 4], BF16, tag="hg", align_bytes=64)
                 state[("hg", c)] = hg
-            gv = state[("hg", c)][:].rearrange("p (r j u e) -> p r j u e", r=4, u=2, e=2)
-            src = state[("ht", c, q)][:].bitcast(BF16).rearrange("p (r u j e) -> p r j u e", r=2, u=2, e=2)
-            for r in tiles:
-                if engine == "s":
-                    nc.scalar.activation(out=gv[:, 2 * q + r], in_=src[:, r], func=ACT.Relu)
-                else:
-                    nc.vector.tensor_scalar(out=gv[:, 2 * q + r], in0=src[:, r], scalar1=0.0, scalar2=None, op0=ALU.max)
+            gv = state[("hg", c)][:].rearrange("p (n u e) -> p n u e", u=2, e=2)
+            src = state[("ht", c, q)][:].bitcast(BF16).rearrange("p (u n e) -> p n u e", u=2, e=2)
+            lo, hi = tiles[0] * P, (tiles[-1] + 1) * P
+            dst = gv[:, 2 * q * P + lo:2 * q * P + hi]
+            if engine == "s":
+                nc.scalar.activation(out=dst, in_=src[:, lo:hi], func=ACT.Relu)
+            else:
+                nc.vector.tensor_scalar(out=dst, in0=src[:, lo:hi], scalar1=0.0, scalar2=None, op0=ALU.max)
 
         def h_quantize(c, tiles):
             if ("h", c) not in state:
@@ -273,6 +274,11 @@ def tile_dynamiclayer_t_kernel(tc, x, W1, b1, W2, b2, Wf, bf, out):
         filler = const.tile([P, D], BF16)
         nc.vector.memset(filler[:], 0.0)
 
+        def keep_warm_in_loop(n):
+            for e in range(n):
+                bank = ps_s.tile([P, D], F32, tag="s", name="bank")
+                nc.tensor.matmul(out=bank[:], lhsT=ones[:], rhs=filler[:], start=True, stop=True)
+
         def keep_warm(n):
             for e in range(n):
                 bank = ps_y.tile([P, D], F32, tag="y", name="bank")
@@ -312,43 +318,48 @@ def tile_dynamiclayer_t_kernel(tc, x, W1, b1, W2, b2, Wf, bf, out):
         for i in range(NCH - 1):
             trn, fin = i >= 1, i >= 2
             enter = i + 2 < NCH
-            x_empty(i + 1, "ss", (0,))
-            if fin:
-                add_bias(i - 2, 1)
-            x_empty(i + 1, "ss", (1,))
             offsets(i + 1)
-            if trn:
-                h_transposes(i - 1, 0)
             short_bias(i, 0)
             short_bias(i, 1)
             short_z(i, 1)
+            x_empty(i + 1, "ss", (0,))
+            if fin:
+                add_bias(i - 2, 0)
+            x_empty(i + 1, "ss", (1,))
+            if fin:
+                add_bias(i - 2, 1)
+            if i == 1:
+                wf_banks = [weight_transposes(wf_sb, q, ps_y, "y") for q in range(2)]
+                for q in range(2):
+                    empty(wf_banks[q], weight_part(gf, q), "s")
             if trn:
+                merge(i - 1)
+                h_transposes(i - 1, 0)
                 h_transposes(i - 1, 1)
                 h_empty(i - 1, 0, "s")
             long_bias(i, 0)
             long_z(i, 2)
-            if fin:
-                last_matmul(i - 2, 2)
             long_bias(i, 1)
             long_z(i, 3)
-            if i == 0:
-                wf_banks = [weight_transposes(wf_sb, q, ps_y, "y") for q in range(2)]
             if i == 1:
                 bf_row = spread_row(D, D, ps_y, "y", "bf_row", False)
             if fin:
+                last_matmul(i - 2, 2)
                 last_matmul(i - 2, 3)
             if enter:
-                x_transposes(i + 2, 0)
-                x_transposes(i + 2, 1)
                 row_sums(i + 2, range(2))
             short_bias(i, 2)
             short_bias(i, 3)
+            if enter:
+                x_transposes(i + 2, 0)
+                keep_warm_in_loop(1)
             long_bias(i, 2)
             if trn:
                 h_empty(i - 1, 1, "v" if enter else "s")
             if fin:
                 add_bias(i - 2, 2)
             if enter:
+                x_transposes(i + 2, 1)
                 row_sums(i + 2, range(2, R))
             x_quantize(i + 1)
             short_z(i + 1, 0)
@@ -365,13 +376,10 @@ def tile_dynamiclayer_t_kernel(tc, x, W1, b1, W2, b2, Wf, bf, out):
                 store(i - 2, range(R))
             if trn:
                 last_matmul(i - 1, 1)
-                add_bias(i - 1, 0)
-            merge(i)
-            if i == 0:
-                for q in range(2):
-                    empty(wf_banks[q], weight_part(gf, q), "ss"[q])
 
         c = NCH - 1
+        merge(c - 1)
+        add_bias(c - 2, 0)
         h_transposes(c - 1, 0)
         short_bias(c, 0)
         short_bias(c, 1)

@@ -164,6 +164,16 @@ def tile_dynamiclayer_t_kernel(tc, x, W1, b1, W2, b2, Wf, bf, out):
                 lo = (h * R + r) * D
                 nc.scalar.activation(out=junk[:], in_=xs[s][:, lo:lo + D], func=ACT.Abs, accum_out=ssum[:, r:r + 1])
 
+        def row_sums_on_vector(c, lo, hi):
+            s, h = c // 2, c % 2
+            if ("s", c) not in state:
+                ssum = work.tile([P, R], F32, tag="ssum")
+                state[("s", c)] = ssum
+            first = (h * R + lo) * D
+            nc.vector.tensor_reduce(out=state[("s", c)][:, lo:hi],
+                                    in_=xs[s][:, first:first + (hi - lo) * D].rearrange("p (r k) -> p r k", k=D),
+                                    axis=mybir.AxisListType.X, op=ALU.add, apply_absolute_value=True)
+
         def offsets(c):
             ssum = state[("s", c)]
             off1 = work.tile([P, R], F32, tag="off1")
@@ -287,27 +297,26 @@ def tile_dynamiclayer_t_kernel(tc, x, W1, b1, W2, b2, Wf, bf, out):
         g1 = weight_tile(U1, "w1")
         g2 = weight_tile(U2, "w2")
         gf = weight_tile(U1, "wf")
-        keep_warm(6)
+        keep_warm(3)
         for q in range(2):
             x_transposes(0, q)
-            keep_warm(1)
-        row_sums(0, range(R))
+        row_sums_on_vector(0, 0, 2)
+        row_sums(0, (2, 3))
         offsets(0)
+        b2_row = spread_row(2 * D, U2, ps_y, "y", "b2_row", True)
+        b1_row = spread_row(0, U1, ps_y, "y", "b1_row", True)
         x_empty(0, "vv")
         w1_banks = []
         for q in range(2):
             w1_banks.append(weight_transposes(w1_sb, q, ps_z, "z"))
-            keep_warm(1)
         w2_bank = weight_transposes(w2_sb, 0, ps_s, "s")
-        keep_warm(1)
+        keep_warm(3)
+        empty_by_pairs(w1_banks[0], g1, 0, "vv")
         x_quantize(0)
-        empty_by_pairs(w1_banks[0], g1, 0, "ss")
-        empty_by_pairs(w1_banks[1], g1, 1, "vv")
+        empty_by_pairs(w1_banks[1], g1, 1, "ss")
         empty_by_pairs(w2_bank, g2, 0, "ss")
         w1q = weight_quantize(g1, U1, "w1")
         w2q = weight_quantize(g2, U2, "w2")
-        b2_row = spread_row(2 * D, U2, ps_y, "y", "b2_row", True)
-        b1_row = spread_row(0, U1, ps_y, "y", "b1_row", True)
         short_z(0, 0)
         long_z(0, 0)
         long_z(0, 1)

@@ -26,7 +26,7 @@ OFF = -3.0e38
 
 
 def pool_tiles(c):
-    return POOL_TILES if c < NCH - 3 else (0,)
+    return POOL_TILES if c < NCH - 3 else ((0,1) if c == NCH - 3 else ((1,) if c==NCH-2 else ()))
 
 
 def tile_dynamiclayer_t_kernel(tc, x, W1, b1, W2, b2, Wf, bf, out):
@@ -47,6 +47,10 @@ def tile_dynamiclayer_t_kernel(tc, x, W1, b1, W2, b2, Wf, bf, out):
         wf_sb = const.tile([P, 4, U1], BF16)
         rows = const.tile([P, ROWS], BF16)
         warm = const.tile([P, 1], F32)
+        ones = const.tile([P, P], BF16)
+        nc.vector.memset(ones[:], 1.0)
+        filler = const.tile([P, D], BF16)
+        nc.vector.memset(filler[:], 0.0)
         nc.vector.memset(rows[:].bitcast(I32), 0)
         nc.vector.memset(warm[:], 0.0)
         nc.scalar.activation(out=warm[:], in_=warm[:], func=ACT.Relu)
@@ -58,20 +62,18 @@ def tile_dynamiclayer_t_kernel(tc, x, W1, b1, W2, b2, Wf, bf, out):
         for s in range(NSUP):
             xt_sb = xpool.tile([P, (SUP // P) * D], BF16, name="x%d" % s)
             xs.append(xt_sb)
-        w1_view = W1.rearrange("(a p) k -> p a k", p=P)
-        for q in range(2):
-            nc.sync.dma_start(out=xs[0][:, q * 2 * D:(q + 1) * 2 * D], in_=x_view[0][:, q * 2 * D:(q + 1) * 2 * D])
+        w1_view = W1.rearrange("(p a) k -> p a k", p=P)
+        nc.sync.dma_start(out=xs[0][:, 0:2 * D], in_=x_view[0][:, 0:2 * D])
         for q in range(2):
             nc.sync.dma_start(out=w1_sb[:, 2 * q:2 * q + 2], in_=w1_view[:, 2 * q:2 * q + 2])
-        nc.sync.dma_start(out=w2_sb[:], in_=W2.rearrange("(a p) k -> p a k", p=P))
+        nc.sync.dma_start(out=w2_sb[:], in_=W2.rearrange("(p a) k -> p a k", p=P))
+        nc.sync.dma_start(out=xs[0][:, 2 * D:4 * D], in_=x_view[0][:, 2 * D:4 * D])
         nc.sync.dma_start(out=xs[0][:, 4 * D:8 * D], in_=x_view[0][:, 4 * D:8 * D])
-        nc.sync.dma_start(out=wf_sb[:], in_=Wf.rearrange("(a p) u -> p a u", p=P))
+        nc.sync.dma_start(out=wf_sb[:], in_=Wf.rearrange("(p a) u -> p a u", p=P))
         for s in range(1, NSUP):
             nc.sync.dma_start(out=xs[s][:], in_=x_view[s])
         ident_f = const.tile([P, P], F32)
         make_identity(nc, ident_f[:])
-        ones = const.tile([P, P], BF16)
-        nc.gpsimd.memset(ones[:], 1.0)
 
         def transposes(bank, srcs):
             for n in range(4):
@@ -97,20 +99,23 @@ def tile_dynamiclayer_t_kernel(tc, x, W1, b1, W2, b2, Wf, bf, out):
         def weight_tile(units, name):
             return const.tile([P, units * 4], BF16, align_bytes=64, name="g_" + name)
 
-        def weight_part(g, q):
-            gv = g[:].bitcast(F32).rearrange("p (a j u) -> p a j u", j=P, u=2)
-            return gv[:, 2 * q:2 * q + 2]
+        def copy_words(dst, src, engine):
+            if engine == "s":
+                nc.scalar.copy(out=dst, in_=src)
+            else:
+                nc.vector.tensor_copy(out=dst, in_=src)
 
-        def empty_by_pairs(bank, g, q, engines):
-            gv = g[:].bitcast(F32).rearrange("p (v m e u) -> p v m e u", v=2, e=2, u=2)
-            bv = bank[:].rearrange("p (r u m v e) -> p r v m e u", r=2, u=2, v=2, e=2)
-            for r in range(2):
-                lo = (2 * q + r) * (P // 4)
-                for v in range(2):
-                    if engines[r] == "s":
-                        nc.scalar.copy(out=gv[:, v, lo:lo + P // 4], in_=bv[:, r, v])
-                    else:
-                        nc.vector.tensor_copy(out=gv[:, v, lo:lo + P // 4], in_=bv[:, r, v])
+        def empty_w1(bank, v, engine):
+            copy_words(g1[:].bitcast(F32).rearrange("p (v m e u) -> p v m e u", v=2, e=2, u=2)[:, v],
+                       bank[:].rearrange("p (e u m) -> p m e u", e=2, u=2), engine)
+
+        def empty_w2(bank, v, engine):
+            copy_words(g2[:].bitcast(F32).rearrange("p (v m e u) -> p v m e u", v=2, e=2, u=2)[:, v],
+                       bank[:].rearrange("p (e u m v) -> p v m e u", e=2, u=2, v=2)[:, v], engine)
+
+        def empty_wf(bank, q, engine):
+            copy_words(gf[:].bitcast(F32).rearrange("p (m a u) -> p m a u", a=4, u=2)[:, :, 2 * q:2 * q + 2],
+                       bank[:].rearrange("p (a u m) -> p m a u", a=2, u=2), engine)
 
         def weight_quantize(g, units, name):
             codes = const.tile([P, units], U32, align_bytes=64, name="c_" + name)
@@ -147,11 +152,15 @@ def tile_dynamiclayer_t_kernel(tc, x, W1, b1, W2, b2, Wf, bf, out):
             for q in banks:
                 empty(state[("t", c, q)], gv[:, 2 * q:2 * q + 2], engines[q])
 
-        def x_quantize(c):
-            xc = work.tile([P, CH], U32, tag="xc", align_bytes=64)
-            xsc = work.tile([P, CH], U8, tag="xsc", align_bytes=64)
-            nc.vector.quantize_mx(out=xc[:].bitcast(FP8X4), scales=xsc[:], in_=state[("g", c)][:])
-            state[("x", c)] = (xc, xsc)
+        def x_quantize(c, tiles=(0, R)):
+            if ("x", c) not in state:
+                xc = work.tile([P, CH], U32, tag="xc", align_bytes=64)
+                xsc = work.tile([P, CH], U8, tag="xsc", align_bytes=64)
+                state[("x", c)] = (xc, xsc)
+            xc, xsc = state[("x", c)]
+            cols = slice(tiles[0] * P, tiles[1] * P)
+            nc.vector.quantize_mx(out=xc[:, cols].bitcast(FP8X4), scales=xsc[:, cols],
+                                  in_=state[("g", c)][:, cols.start * 4:cols.stop * 4])
 
         def row_sums(c, tiles):
             s, h = c // 2, c % 2
@@ -174,13 +183,14 @@ def tile_dynamiclayer_t_kernel(tc, x, W1, b1, W2, b2, Wf, bf, out):
                                     in_=xs[s][:, first:first + (hi - lo) * D].rearrange("p (r k) -> p r k", k=D),
                                     axis=mybir.AxisListType.X, op=ALU.add, apply_absolute_value=True)
 
-        def offsets(c):
-            ssum = state[("s", c)]
-            off1 = work.tile([P, R], F32, tag="off1")
-            off2 = work.tile([P, R], F32, tag="off2")
-            nc.gpsimd.tensor_scalar(out=off1[:], in0=ssum[:], scalar1=float(D), scalar2=OFF, op0=ALU.is_le, op1=ALU.mult)
-            nc.gpsimd.tensor_scalar(out=off2[:], in0=ssum[:], scalar1=float(D), scalar2=OFF, op0=ALU.is_gt, op1=ALU.mult)
-            state[("off", c)] = (off1, off2)
+        def offsets(c, lo=0, hi=R):
+            if ("off", c) not in state:
+                off1 = work.tile([P, R], F32, tag="off1")
+                off2 = work.tile([P, R], F32, tag="off2")
+                state[("off", c)] = (off1, off2)
+            ssum = state[("s", c)][:, lo:hi]
+            for off, op in zip(state[("off", c)], (ALU.is_le, ALU.is_gt)):
+                nc.gpsimd.tensor_scalar(out=off[:, lo:hi], in0=ssum, scalar1=float(D), scalar2=OFF, op0=op, op1=ALU.mult)
 
         def x_tile(c, r):
             xc, xsc = state[("x", c)]
@@ -281,9 +291,6 @@ def tile_dynamiclayer_t_kernel(tc, x, W1, b1, W2, b2, Wf, bf, out):
             lo, hi = tiles[0] * D, (tiles[-1] + 1) * D
             nc.sync.dma_start(out=out_view[s][:, h * R * D + lo:h * R * D + hi], in_=state[("o", c)][:, lo:hi])
 
-        filler = const.tile([P, D], BF16)
-        nc.vector.memset(filler[:], 0.0)
-
         def keep_warm_in_loop(n):
             for e in range(n):
                 bank = ps_s.tile([P, D], F32, tag="s", name="bank")
@@ -297,31 +304,36 @@ def tile_dynamiclayer_t_kernel(tc, x, W1, b1, W2, b2, Wf, bf, out):
         g1 = weight_tile(U1, "w1")
         g2 = weight_tile(U2, "w2")
         gf = weight_tile(U1, "wf")
-        keep_warm(3)
-        for q in range(2):
-            x_transposes(0, q)
+        keep_warm(8)
+        x_transposes(0, 0)
         row_sums_on_vector(0, 0, 2)
-        row_sums(0, (2, 3))
-        offsets(0)
+        x_empty(0, "v", (0,))
+        w1_banks = [weight_transposes(w1_sb, 0, ps_z, "z")]
+        keep_warm(0)
+        w1_banks.append(weight_transposes(w1_sb, 1, ps_z, "z"))
+        empty_w1(w1_banks[0], 0, "s")
         b2_row = spread_row(2 * D, U2, ps_y, "y", "b2_row", True)
         b1_row = spread_row(0, U1, ps_y, "y", "b1_row", True)
-        x_empty(0, "vv")
-        w1_banks = []
-        for q in range(2):
-            w1_banks.append(weight_transposes(w1_sb, q, ps_z, "z"))
+        keep_warm(0)
         w2_bank = weight_transposes(w2_sb, 0, ps_s, "s")
-        keep_warm(3)
-        empty_by_pairs(w1_banks[0], g1, 0, "vv")
-        x_quantize(0)
-        empty_by_pairs(w1_banks[1], g1, 1, "ss")
-        empty_by_pairs(w2_bank, g2, 0, "ss")
+        x_quantize(0, (0, 2))
+        empty_w1(w1_banks[1], 1, "v")
+        empty_w2(w2_bank, 0, "s")
+        empty_w2(w2_bank, 1, "s")
+        x_transposes(0, 1)
+        offsets(0, 0, 2)
+        keep_warm(1)
         w1q = weight_quantize(g1, U1, "w1")
         w2q = weight_quantize(g2, U2, "w2")
-        short_z(0, 0)
         long_z(0, 0)
         long_z(0, 1)
+        short_z(0, 0)
+        x_empty(0, "vv", (1,))
+        x_quantize(0, (2, 4))
         x_transposes(1, 0)
         x_transposes(1, 1)
+        row_sums(0, (2, 3))
+        offsets(0, 2, R)
         row_sums(1, range(R))
 
         for i in range(NCH - 1):
@@ -340,7 +352,7 @@ def tile_dynamiclayer_t_kernel(tc, x, W1, b1, W2, b2, Wf, bf, out):
             if i == 1:
                 wf_banks = [weight_transposes(wf_sb, q, ps_y, "y") for q in range(2)]
                 for q in range(2):
-                    empty(wf_banks[q], weight_part(gf, q), "s")
+                    empty_wf(wf_banks[q], q, "s")
             if trn:
                 merge(i - 1)
                 h_transposes(i - 1, 0)
@@ -354,14 +366,18 @@ def tile_dynamiclayer_t_kernel(tc, x, W1, b1, W2, b2, Wf, bf, out):
                 bf_row = spread_row(D, D, ps_y, "y", "bf_row", False)
             if fin:
                 last_matmul(i - 2, 2)
-                last_matmul(i - 2, 3)
+                if not enter:
+                    last_matmul(i - 2, 3)
             if enter:
                 row_sums(i + 2, range(2))
             short_bias(i, 2)
             short_bias(i, 3)
             if enter:
                 x_transposes(i + 2, 0)
-                keep_warm_in_loop(1)
+                if fin:
+                    last_matmul(i - 2, 3)
+                else:
+                    keep_warm_in_loop(1)
             long_bias(i, 2)
             if trn:
                 h_empty(i - 1, 1, "v" if enter else "s")
@@ -390,53 +406,58 @@ def tile_dynamiclayer_t_kernel(tc, x, W1, b1, W2, b2, Wf, bf, out):
         merge(c - 1)
         add_bias(c - 2, 0)
         h_transposes(c - 1, 0)
+        h_transposes(c - 1, 1)
+        add_bias(c - 2, 1)
+        store(c - 2, (0, 1))
+        last_matmul(c - 2, 2)
         short_bias(c, 0)
         short_bias(c, 1)
         short_z(c, 1)
-        h_transposes(c - 1, 1)
+        last_matmul(c - 2, 3)
         h_empty(c - 1, 0, "s")
-        h_empty(c - 1, 1, "s")
         long_bias(c, 0)
         long_z(c, 2)
-        last_matmul(c - 2, 2)
         long_bias(c, 1)
         long_z(c, 3)
-        add_bias(c - 2, 1)
-        store(c - 2, (0, 1))
-        last_matmul(c - 2, 3)
-        merge(c, (0, 2))
-        h_transposes(c, 0)
-        h_empty(c, 0, "s")
+        h_empty(c - 1, 1, "s")
+        add_bias(c - 2, 2)
         short_bias(c, 2)
         short_bias(c, 3)
-        h_quantize(c - 1, (0, 1, 2, 3))
-        last_matmul(c - 1, 0, ps_s)
+        merge(c, (0, 2))
+        h_transposes(c, 0)
         long_bias(c, 2)
-        last_matmul(c - 1, 1, ps_z)
+        h_empty(c, 0, "s")
+        h_quantize(c - 1, (0, 1, 2, 3))
+        last_matmul(c - 1, 0)
         long_bias(c, 3)
+        last_matmul(c - 1, 1, ps_z)
         last_matmul(c - 1, 2, ps_z)
-        add_bias(c - 1, 0)
-        add_bias(c - 2, 2)
-        last_matmul(c - 1, 3)
         add_bias(c - 2, 3)
         store(c - 2, (2, 3))
-        add_bias(c - 1, 1)
-        store(c - 1, (0, 1))
+        last_matmul(c - 1, 3)
         merge(c, (2, R))
         h_transposes(c, 1)
+        add_bias(c - 1, 0)
+        store(c - 1, (0,))
+        add_bias(c - 1, 1)
+        store(c - 1, (1,))
         h_quantize(c, (0, 1))
-        last_matmul(c, 0)
-        last_matmul(c, 1, ps_s)
-        h_empty(c, 1, "s", (0,))
+        last_matmul(c, 0, ps_s)
+        last_matmul(c, 1, ps_z)
         add_bias(c - 1, 2)
         store(c - 1, (2,))
+        h_empty(c, 1, "s", (0,))
         h_empty(c, 1, "v", (1,))
         add_bias(c - 1, 3)
         store(c - 1, (3,))
+        add_bias(c, 0)
+        store(c, (0,))
         h_quantize(c, (2, 3))
-        last_matmul(c, 2, ps_z)
-        last_matmul(c, 3, ps_z)
-        for r in range(R):
-            add_bias(c, r)
-        for r in (1, 2, 0, 3):
-            store(c, (r,))
+        last_matmul(c, 2)
+        last_matmul(c, 3)
+        add_bias(c, 1)
+        store(c, (1,))
+        add_bias(c, 2)
+        store(c, (2,))
+        add_bias(c, 3)
+        store(c, (3,))

@@ -291,11 +291,6 @@ def tile_dynamiclayer_t_kernel(tc, x, W1, b1, W2, b2, Wf, bf, out):
             lo, hi = tiles[0] * D, (tiles[-1] + 1) * D
             nc.sync.dma_start(out=out_view[s][:, h * R * D + lo:h * R * D + hi], in_=state[("o", c)][:, lo:hi])
 
-        def keep_warm_in_loop(n):
-            for e in range(n):
-                bank = ps_s.tile([P, D], F32, tag="s", name="bank")
-                nc.tensor.matmul(out=bank[:], lhsT=ones[:], rhs=filler[:], start=True, stop=True)
-
         def keep_warm(n):
             for e in range(n):
                 bank = ps_y.tile([P, D], F32, tag="y", name="bank")
@@ -357,6 +352,9 @@ def tile_dynamiclayer_t_kernel(tc, x, W1, b1, W2, b2, Wf, bf, out):
                 merge(i - 1)
                 h_transposes(i - 1, 0)
                 h_transposes(i - 1, 1)
+            if enter:
+                row_sums(i + 2, range(1))
+            if trn:
                 h_empty(i - 1, 0, "s")
             long_bias(i, 0)
             long_z(i, 2)
@@ -369,18 +367,16 @@ def tile_dynamiclayer_t_kernel(tc, x, W1, b1, W2, b2, Wf, bf, out):
                 if not enter:
                     last_matmul(i - 2, 3)
             if enter:
-                row_sums(i + 2, range(2))
+                row_sums(i + 2, range(1, 2))
             short_bias(i, 2)
             short_bias(i, 3)
             if enter:
                 x_transposes(i + 2, 0)
                 if fin:
                     last_matmul(i - 2, 3)
-                else:
-                    keep_warm_in_loop(1)
-            long_bias(i, 2)
             if trn:
                 h_empty(i - 1, 1, "v" if enter else "s")
+            long_bias(i, 2)
             if fin:
                 add_bias(i - 2, 2)
             if enter:

@@ -173,16 +173,6 @@ def tile_dynamiclayer_t_kernel(tc, x, W1, b1, W2, b2, Wf, bf, out):
                 lo = (h * R + r) * D
                 nc.scalar.activation(out=junk[:], in_=xs[s][:, lo:lo + D], func=ACT.Abs, accum_out=ssum[:, r:r + 1])
 
-        def row_sums_on_vector(c, lo, hi):
-            s, h = c // 2, c % 2
-            if ("s", c) not in state:
-                ssum = work.tile([P, R], F32, tag="ssum")
-                state[("s", c)] = ssum
-            first = (h * R + lo) * D
-            nc.vector.tensor_reduce(out=state[("s", c)][:, lo:hi],
-                                    in_=xs[s][:, first:first + (hi - lo) * D].rearrange("p (r k) -> p r k", k=D),
-                                    axis=mybir.AxisListType.X, op=ALU.add, apply_absolute_value=True)
-
         def offsets(c, lo=0, hi=R):
             if ("off", c) not in state:
                 off1 = work.tile([P, R], F32, tag="off1")
@@ -301,7 +291,7 @@ def tile_dynamiclayer_t_kernel(tc, x, W1, b1, W2, b2, Wf, bf, out):
         gf = weight_tile(U1, "wf")
         keep_warm(8)
         x_transposes(0, 0)
-        row_sums_on_vector(0, 0, 2)
+        row_sums(0, (0, 1))
         x_empty(0, "v", (0,))
         w1_banks = [weight_transposes(w1_sb, 0, ps_z, "z")]
         keep_warm(0)
@@ -319,17 +309,21 @@ def tile_dynamiclayer_t_kernel(tc, x, W1, b1, W2, b2, Wf, bf, out):
         offsets(0, 0, 2)
         keep_warm(1)
         w1q = weight_quantize(g1, U1, "w1")
-        w2q = weight_quantize(g2, U2, "w2")
         long_z(0, 0)
         long_z(0, 1)
-        short_z(0, 0)
         x_empty(0, "vv", (1,))
+        w2q = weight_quantize(g2, U2, "w2")
+        short_z(0, 0)
         x_quantize(0, (2, 4))
+        long_bias(0, 0)
+        long_bias(0, 1)
         x_transposes(1, 0)
         x_transposes(1, 1)
         row_sums(0, (2, 3))
         offsets(0, 2, R)
-        row_sums(1, range(R))
+        row_sums(1, (0, 1))
+        x_empty(1, "ss", (0,))
+        row_sums(1, (2, 3))
 
         for i in range(NCH - 1):
             trn, fin = i >= 1, i >= 2
@@ -338,10 +332,11 @@ def tile_dynamiclayer_t_kernel(tc, x, W1, b1, W2, b2, Wf, bf, out):
             short_bias(i, 0)
             short_bias(i, 1)
             short_z(i, 1)
-            x_empty(i + 1, "ss", (0,))
+            if i >= 1:
+                x_empty(i + 1, "ss", (0,))
             if fin:
                 add_bias(i - 2, 0)
-            x_empty(i + 1, "ss", (1,))
+            x_empty(i + 1, "ss" if i >= 1 else "vv", (1,))
             if fin:
                 add_bias(i - 2, 1)
             if i == 1:
@@ -356,9 +351,11 @@ def tile_dynamiclayer_t_kernel(tc, x, W1, b1, W2, b2, Wf, bf, out):
                 row_sums(i + 2, range(1))
             if trn:
                 h_empty(i - 1, 0, "s")
-            long_bias(i, 0)
+            if i >= 1:
+                long_bias(i, 0)
             long_z(i, 2)
-            long_bias(i, 1)
+            if i >= 1:
+                long_bias(i, 1)
             long_z(i, 3)
             if i == 1:
                 bf_row = spread_row(D, D, ps_y, "y", "bf_row", False)
@@ -371,16 +368,16 @@ def tile_dynamiclayer_t_kernel(tc, x, W1, b1, W2, b2, Wf, bf, out):
             short_bias(i, 2)
             short_bias(i, 3)
             if enter:
-                x_transposes(i + 2, 0)
                 if fin:
                     last_matmul(i - 2, 3)
+                x_transposes(i + 2, 0)
+                x_transposes(i + 2, 1)
             if trn:
                 h_empty(i - 1, 1, "v" if enter else "s")
             long_bias(i, 2)
             if fin:
                 add_bias(i - 2, 2)
             if enter:
-                x_transposes(i + 2, 1)
                 row_sums(i + 2, range(2, R))
             x_quantize(i + 1)
             short_z(i + 1, 0)

@@ -126,7 +126,7 @@ def tile_dynamiclayer_t_kernel(tc, x, W1, b1, W2, b2, Wf, bf, out):
         def spread_row(lo, width, pool, tag, name, by_pairs):
             bank = pool.tile([P, 512], F32, tag=tag, name="bank")
             nc.tensor.matmul(out=bank[:, 0:width], lhsT=ones[:], rhs=rows[:, lo:lo + width], start=True, stop=True)
-            row = const.tile([P, width], BF16, name=name)
+            row = const.tile([P, width], F32, name=name)
             if by_pairs:
                 nc.scalar.copy(out=row[:].rearrange("p (v m e) -> p v m e", v=2, e=2),
                                in_=bank[:, 0:width].rearrange("p (m v e) -> p v m e", v=2, e=2))

from contextlib import ExitStack

import concourse.mybir as mybir
from concourse.masks import make_identity

F32 = mybir.dt.float32
BF16 = mybir.dt.bfloat16
I32 = mybir.dt.int32
U32 = mybir.dt.uint32
U8 = mybir.dt.uint8
FP8X4 = mybir.dt.float8_e4m3fn_x4
ALU = mybir.AluOpType
ACT = mybir.ActivationFunctionType

P = 128
B, D, U1, U2 = 8192, 512, 512, 256
FLOPS = 2 * B * D * (U1 + U2) + 2 * B * U1 * D
CH = 512
R = CH // P
NCH = B // CH
POOL_TILES = (0, 1, 2)
SUP = 1024
NSUP = B // SUP
ROWS = U1 + D + U2
OFF = -3.0e38


def pool_tiles(c):
    return POOL_TILES if c < NCH - 3 else ((0,1) if c == NCH - 3 else ((1,) if c==NCH-2 else ()))


def tile_dynamiclayer_t_kernel(tc, x, W1, b1, W2, b2, Wf, bf, out):
    nc = tc.nc
    with ExitStack() as ctx:
        const = ctx.enter_context(tc.tile_pool(name="const", bufs=1))
        xpool = ctx.enter_context(tc.tile_pool(name="xpool", bufs=1))
        work = ctx.enter_context(tc.tile_pool(name="work", bufs=3))
        opool = ctx.enter_context(tc.tile_pool(name="opool", bufs=3))
        ps_t = ctx.enter_context(tc.psum_pool(name="ps_t", bufs=3))
        ps_z = ctx.enter_context(tc.psum_pool(name="ps_z", bufs=2))
        ps_s = ctx.enter_context(tc.psum_pool(name="ps_s", bufs=1))
        ps_y = ctx.enter_context(tc.psum_pool(name="ps_y", bufs=2))
        ctx.enter_context(tc.manual_schedule())

        w1_sb = const.tile([P, 4, D], BF16)
        w2_sb = const.tile([P, 2, D], BF16)
        wf_sb = const.tile([P, 4, U1], BF16)
        rows = const.tile([P, ROWS], BF16)
        warm = const.tile([P, 1], F32)
        ones = const.tile([P, P], BF16)
        nc.vector.memset(ones[:], 1.0)
        filler = const.tile([P, D], BF16)
        nc.vector.memset(filler[:], 0.0)
        nc.vector.memset(rows[:].bitcast(I32), 0)
        nc.vector.memset(warm[:], 0.0)
        nc.scalar.activation(out=warm[:], in_=warm[:], func=ACT.Relu)
        nc.scalar.dma_start(out=rows[0:1, 2 * D:ROWS], in_=b2.unsqueeze(0))
        nc.scalar.dma_start(out=rows[0:1, 0:D], in_=b1.unsqueeze(0))
        nc.scalar.dma_start(out=rows[0:1, D:2 * D], in_=bf.unsqueeze(0))
        x_view = x.rearrange("(s p r) k -> s p (r k)", p=P, r=SUP // P)
        xs = []
        for s in range(NSUP):
            xt_sb = xpool.tile([P, (SUP // P) * D], BF16, name="x%d" % s)
            xs.append(xt_sb)
        w1_view = W1.rearrange("(p a) k -> p a k", p=P)
        nc.sync.dma_start(out=xs[0][:, 0:2 * D], in_=x_view[0][:, 0:2 * D])
        for q in range(2):
            nc.sync.dma_start(out=w1_sb[:, 2 * q:2 * q + 2], in_=w1_view[:, 2 * q:2 * q + 2])
        nc.sync.dma_start(out=w2_sb[:], in_=W2.rearrange("(p a) k -> p a k", p=P))
        nc.sync.dma_start(out=xs[0][:, 2 * D:4 * D], in_=x_view[0][:, 2 * D:4 * D])
        nc.sync.dma_start(out=xs[0][:, 4 * D:8 * D], in_=x_view[0][:, 4 * D:8 * D])
        nc.sync.dma_start(out=wf_sb[:], in_=Wf.rearrange("(p a) u -> p a u", p=P))
        for s in range(1, NSUP):
            nc.sync.dma_start(out=xs[s][:], in_=x_view[s])
        ident_f = const.tile([P, P], F32)
        make_identity(nc, ident_f[:])

        def transposes(bank, srcs):
            for n in range(4):
                nc.tensor.transpose(bank[:, n * P:(n + 1) * P], srcs[n], ident_f[:])

        def empty(bank, dst, engine):
            src = bank[:].rearrange("p (r u j) -> p r j u", r=2, u=2)
            if engine == "s":
                nc.scalar.copy(out=dst, in_=src)
            else:
                nc.vector.tensor_copy(out=dst, in_=src)

        def words(flat_f32, tile_index):
            lo = tile_index * 256
            return [flat_f32[:, lo:lo + 256:2], flat_f32[:, lo + 1:lo + 256:2]]

        def weight_transposes(w_sb, q, pool, tag):
            wv = w_sb[:].rearrange("p a k -> p (a k)").bitcast(F32)
            bank = pool.tile([P, 512], F32, tag=tag, name="bank")
            transposes(bank, words(wv, 2 * q) + words(wv, 2 * q + 1))
            return bank

        def weight_tile(units, name):
            return const.tile([P, units * 4], BF16, align_bytes=64, name="g_" + name)

        def copy_words(dst, src, engine):
            if engine == "s":
                nc.scalar.copy(out=dst, in_=src)
            else:
                nc.vector.tensor_copy(out=dst, in_=src)

        def empty_w1(bank, v, engine):
            copy_words(g1[:].bitcast(F32).rearrange("p (v m e u) -> p v m e u", v=2, e=2, u=2)[:, v],
                       bank[:].rearrange("p (e u m) -> p m e u", e=2, u=2), engine)

        def empty_w2(bank, v, engine):
            copy_words(g2[:].bitcast(F32).rearrange("p (v m e u) -> p v m e u", v=2, e=2, u=2)[:, v],
                       bank[:].rearrange("p (e u m v) -> p v m e u", e=2, u=2, v=2)[:, v], engine)

        def empty_wf(bank, q, engine):
            copy_words(gf[:].bitcast(F32).rearrange("p (m a u) -> p m a u", a=4, u=2)[:, :, 2 * q:2 * q + 2],
                       bank[:].rearrange("p (a u m) -> p m a u", a=2, u=2), engine)

        def weight_quantize(g, units, name):
            codes = const.tile([P, units], U32, align_bytes=64, name="c_" + name)
            scales = const.tile([P, units], U8, align_bytes=64, name="s_" + name)
            nc.vector.quantize_mx(out=codes[:].bitcast(FP8X4), scales=scales[:], in_=g[:])
            return codes[:].bitcast(FP8X4), scales[:]

        def spread_row(lo, width, pool, tag, name, by_pairs):
            bank = pool.tile([P, 512], F32, tag=tag, name="bank")
            nc.tensor.matmul(out=bank[:, 0:width], lhsT=ones[:], rhs=rows[:, lo:lo + width], start=True, stop=True)
            row = const.tile([P, width], F32, name=name)
            if by_pairs:
                nc.scalar.copy(out=row[:].rearrange("p (v m e) -> p v m e", v=2, e=2),
                               in_=bank[:, 0:width].rearrange("p (m v e) -> p v m e", v=2, e=2))
            else:
                nc.scalar.copy(out=row[:], in_=bank[:, 0:width])
            return row

        state = {}
        TAGS = {ps_y: "y", ps_z: "z", ps_s: "s"}

        def x_transposes(c, q):
            s, h = c // 2, c % 2
            xv = xs[s][:, h * 4 * D:(h + 1) * 4 * D].bitcast(F32)
            bank = ps_t.tile([P, 512], F32, tag="t", name="bank")
            transposes(bank, words(xv, 2 * q) + words(xv, 2 * q + 1))
            state[("t", c, q)] = bank

        def x_empty(c, engines, banks=(0, 1)):
            if ("g", c) not in state:
                xg = work.tile([P, CH * 4], BF16, tag="xg", align_bytes=64)
                state[("g", c)] = xg
            gv = state[("g", c)][:].bitcast(F32).rearrange("p (r j u) -> p r j u", r=4, u=2)
            for q in banks:
                empty(state[("t", c, q)], gv[:, 2 * q:2 * q + 2], engines[q])

        def x_quantize(c, tiles=(0, R)):
            if ("x", c) not in state:
                xc = work.tile([P, CH], U32, tag="xc", align_bytes=64)
                xsc = work.tile([P, CH], U8, tag="xsc", align_bytes=64)
                state[("x", c)] = (xc, xsc)
            xc, xsc = state[("x", c)]
            cols = slice(tiles[0] * P, tiles[1] * P)
            nc.vector.quantize_mx(out=xc[:, cols].bitcast(FP8X4), scales=xsc[:, cols],
                                  in_=state[("g", c)][:, cols.start * 4:cols.stop * 4])

        def row_sums(c, tiles):
            s, h = c // 2, c % 2
            if ("s", c) not in state:
                ssum = work.tile([P, R], F32, tag="ssum")
                state[("s", c)] = ssum
            ssum = state[("s", c)]
            for r in tiles:
                junk = work.tile([P, D], BF16, tag="junk")
                lo = (h * R + r) * D
                nc.scalar.activation(out=junk[:], in_=xs[s][:, lo:lo + D], func=ACT.Abs, accum_out=ssum[:, r:r + 1])

        def offsets(c, lo=0, hi=R):
            if ("off", c) not in state:
                off1 = work.tile([P, R], F32, tag="off1")
                off2 = work.tile([P, R], F32, tag="off2")
                state[("off", c)] = (off1, off2)
            ssum = state[("s", c)][:, lo:hi]
            for off, op in zip(state[("off", c)], (ALU.is_le, ALU.is_gt)):
                nc.gpsimd.tensor_scalar(out=off[:, lo:hi], in0=ssum, scalar1=float(D), scalar2=OFF, op0=op, op1=ALU.mult)

        def x_tile(c, r):
            xc, xsc = state[("x", c)]
            return xc[:, r * P:(r + 1) * P].bitcast(FP8X4), xsc[:, r * P:(r + 1) * P]

        def long_z(c, r):
            z = ps_z.tile([P, U1], F32, tag="z")
            xc, xsc = x_tile(c, r)
            nc.tensor.matmul_mx(out=z[:], lhsT=xc, lhsT_scale=xsc, rhs=w1q[0], rhs_scale=w1q[1], start=True, stop=True)
            state[("z", c, r)] = z

        def short_z(c, q):
            z = ps_s.tile([P, 2 * U2], F32, tag="s")
            for e in range(2):
                xc, xsc = x_tile(c, 2 * q + e)
                nc.tensor.matmul_mx(out=z[:, e * U2:(e + 1) * U2], lhsT=xc, lhsT_scale=xsc,
                                    rhs=w2q[0], rhs_scale=w2q[1], start=True, stop=True)
            state[("zs", c, q)] = z

        def long_bias(c, r):
            if r == 0:
                h1 = work.tile([P, R * U1], BF16, tag="h1")
                state[("h1", c)] = h1
            nc.vector.scalar_tensor_tensor(out=state[("h1", c)][:, r * U1:(r + 1) * U1], in0=state[("z", c, r)][:],
                                           scalar=state[("off", c)][0][:, r:r + 1], in1=b1_row[:],
                                           op0=ALU.add, op1=ALU.add)

        def short_bias(c, r):
            if r == 0:
                h2 = work.tile([P, R * U2], BF16, tag="h2")
                state[("h2", c)] = h2
            e = r % 2
            nc.vector.scalar_tensor_tensor(out=state[("h2", c)][:, r * U2:(r + 1) * U2],
                                           in0=state[("zs", c, r // 2)][:, e * U2:(e + 1) * U2],
                                           scalar=state[("off", c)][1][:, r:r + 1], in1=b2_row[:],
                                           op0=ALU.add, op1=ALU.add)

        def merge(c, tiles=(0, R)):
            runs = slice(2 * tiles[0], 2 * tiles[1])
            low = state[("h1", c)][:].rearrange("p (g n) -> p g n", g=2 * R)[:, runs, 0:U2 // 2]
            nc.vector.tensor_tensor(out=low, in0=low,
                                    in1=state[("h2", c)][:].rearrange("p (g n) -> p g n", g=2 * R)[:, runs],
                                    op=ALU.max)

        def h_transposes(c, q):
            hv = state[("h1", c)][:].bitcast(F32)
            bank = ps_t.tile([P, 512], F32, tag="t", name="bank")
            transposes(bank, [hv[:, (4 * q + 2 * r + u) * P:(4 * q + 2 * r + u + 1) * P] for u in range(2) for r in range(2)])
            state[("ht", c, q)] = bank

        def h_empty(c, q, engine, tiles=(0, 1)):
            if ("hg", c) not in state:
                hg = work.tile([P, CH * 4], BF16, tag="hg", align_bytes=64)
                state[("hg", c)] = hg
            gv = state[("hg", c)][:].rearrange("p (n u e) -> p n u e", u=2, e=2)
            src = state[("ht", c, q)][:].bitcast(BF16).rearrange("p (u n e) -> p n u e", u=2, e=2)
            lo, hi = tiles[0] * P, (tiles[-1] + 1) * P
            dst = gv[:, 2 * q * P + lo:2 * q * P + hi]
            if engine == "s":
                nc.scalar.activation(out=dst, in_=src[:, lo:hi], func=ACT.Relu)
            else:
                nc.vector.tensor_scalar(out=dst, in0=src[:, lo:hi], scalar1=0.0, scalar2=None, op0=ALU.max)

        def h_quantize(c, tiles):
            if ("h", c) not in state:
                hc = work.tile([P, CH], U32, tag="hc", align_bytes=64)
                hs = work.tile([P, CH], U8, tag="hs", align_bytes=64)
                state[("h", c)] = (hc, hs)
            hc, hs = state[("h", c)]
            cols = slice(tiles[0] * P, (tiles[-1] + 1) * P)
            nc.vector.quantize_mx(out=hc[:, cols].bitcast(FP8X4), scales=hs[:, cols],
                                  in_=state[("hg", c)][:, cols.start * 4:cols.stop * 4])

        out_view = out.rearrange("(s p r) d -> s p (r d)", p=P, r=SUP // P)

        def last_matmul(c, r, pool=ps_y):
            hc, hs = state[("h", c)]
            y = pool.tile([P, D], F32, tag=TAGS[pool], name="y")
            nc.tensor.matmul_mx(out=y[:], lhsT=hc[:, r * P:(r + 1) * P].bitcast(FP8X4),
                                lhsT_scale=hs[:, r * P:(r + 1) * P],
                                rhs=wfq[0], rhs_scale=wfq[1], start=True, stop=True)
            state[("y", c, r)] = y

        def add_bias(c, r):
            if ("o", c) not in state:
                osb = opool.tile([P, R * D], F32, tag="osb")
                state[("o", c)] = osb
            osb = state[("o", c)]
            part = osb[:, r * D:(r + 1) * D]
            if r in pool_tiles(c):
                nc.scalar.copy(out=part, in_=state[("y", c, r)][:])
                nc.gpsimd.tensor_tensor(out=part, in0=part, in1=bf_row[:], op=ALU.add)
            else:
                nc.vector.tensor_tensor(out=part, in0=state[("y", c, r)][:], in1=bf_row[:], op=ALU.add)

        def store(c, tiles):
            s, h = c // 2, c % 2
            lo, hi = tiles[0] * D, (tiles[-1] + 1) * D
            nc.sync.dma_start(out=out_view[s][:, h * R * D + lo:h * R * D + hi], in_=state[("o", c)][:, lo:hi])

        def keep_warm(n):
            for e in range(n):
                bank = ps_y.tile([P, D], F32, tag="y", name="bank")
                nc.tensor.matmul(out=bank[:], lhsT=ones[:], rhs=filler[:], start=True, stop=True)

        g1 = weight_tile(U1, "w1")
        g2 = weight_tile(U2, "w2")
        gf = weight_tile(U1, "wf")
        keep_warm(8)
        x_transposes(0, 0)
        row_sums(0, (0, 1))
        x_empty(0, "v", (0,))
        w1_banks = [weight_transposes(w1_sb, 0, ps_z, "z")]
        keep_warm(0)
        w1_banks.append(weight_transposes(w1_sb, 1, ps_z, "z"))
        empty_w1(w1_banks[0], 0, "s")
        b2_row = spread_row(2 * D, U2, ps_y, "y", "b2_row", True)
        b1_row = spread_row(0, U1, ps_y, "y", "b1_row", True)
        keep_warm(0)
        w2_bank = weight_transposes(w2_sb, 0, ps_s, "s")
        x_quantize(0, (0, 2))
        empty_w1(w1_banks[1], 1, "v")
        empty_w2(w2_bank, 0, "s")
        empty_w2(w2_bank, 1, "s")
        x_transposes(0, 1)
        offsets(0, 0, 2)
        keep_warm(1)
        w1q = weight_quantize(g1, U1, "w1")
        long_z(0, 0)
        long_z(0, 1)
        x_empty(0, "vv", (1,))
        w2q = weight_quantize(g2, U2, "w2")
        short_z(0, 0)
        x_quantize(0, (2, 4))
        long_bias(0, 0)
        long_bias(0, 1)
        x_transposes(1, 0)
        x_transposes(1, 1)
        row_sums(0, (2, 3))
        offsets(0, 2, R)
        row_sums(1, (0, 1))
        x_empty(1, "ss", (0,))
        row_sums(1, (2, 3))

        for i in range(NCH - 1):
            trn, fin = i >= 1, i >= 2
            enter = i + 2 < NCH
            offsets(i + 1)
            short_bias(i, 0)
            short_bias(i, 1)
            short_z(i, 1)
            if i >= 1:
                x_empty(i + 1, "ss", (0,))
            if fin:
                add_bias(i - 2, 0)
            x_empty(i + 1, "ss" if i >= 1 else "vv", (1,))
            if fin:
                add_bias(i - 2, 1)
            if i == 1:
                wf_banks = [weight_transposes(wf_sb, q, ps_y, "y") for q in range(2)]
                for q in range(2):
                    empty_wf(wf_banks[q], q, "s")
            if trn:
                merge(i - 1)
                h_transposes(i - 1, 0)
                h_transposes(i - 1, 1)
            if enter:
                row_sums(i + 2, range(1))
            if trn:
                h_empty(i - 1, 0, "s")
            if i >= 1:
                long_bias(i, 0)
            long_z(i, 2)
            if i >= 1:
                long_bias(i, 1)
            long_z(i, 3)
            if i == 1:
                bf_row = spread_row(D, D, ps_y, "y", "bf_row", False)
            if fin:
                last_matmul(i - 2, 2)
                if not enter:
                    last_matmul(i - 2, 3)
            if enter:
                row_sums(i + 2, range(1, 2))
            short_bias(i, 2)
            short_bias(i, 3)
            if enter:
                if fin:
                    last_matmul(i - 2, 3)
                x_transposes(i + 2, 0)
                x_transposes(i + 2, 1)
            if trn:
                h_empty(i - 1, 1, "v" if enter else "s")
            long_bias(i, 2)
            if fin:
                add_bias(i - 2, 2)
            if enter:
                row_sums(i + 2, range(2, R))
            x_quantize(i + 1)
            short_z(i + 1, 0)
            long_z(i + 1, 0)
            if i == 1:
                wfq = weight_quantize(gf, U1, "wf")
            if trn:
                h_quantize(i - 1, (0, 1, 2, 3))
                last_matmul(i - 1, 0)
            long_bias(i, 3)
            long_z(i + 1, 1)
            if fin:
                add_bias(i - 2, 3)
                store(i - 2, range(R))
            if trn:
                last_matmul(i - 1, 1)

        c = NCH - 1
        merge(c - 1)
        add_bias(c - 2, 0)
        h_transposes(c - 1, 0)
        h_transposes(c - 1, 1)
        add_bias(c - 2, 1)
        store(c - 2, (0, 1))
        last_matmul(c - 2, 2)
        short_bias(c, 0)
        short_bias(c, 1)
        short_z(c, 1)
        last_matmul(c - 2, 3)
        h_empty(c - 1, 0, "s")
        long_bias(c, 0)
        long_z(c, 2)
        long_bias(c, 1)
        long_z(c, 3)
        h_empty(c - 1, 1, "s")
        add_bias(c - 2, 2)
        short_bias(c, 2)
        short_bias(c, 3)
        merge(c, (0, 2))
        h_transposes(c, 0)
        long_bias(c, 2)
        h_empty(c, 0, "s")
        h_quantize(c - 1, (0, 1, 2, 3))
        last_matmul(c - 1, 0)
        long_bias(c, 3)
        last_matmul(c - 1, 1, ps_z)
        last_matmul(c - 1, 2, ps_z)
        add_bias(c - 2, 3)
        store(c - 2, (2, 3))
        last_matmul(c - 1, 3)
        merge(c, (2, R))
        h_transposes(c, 1)
        add_bias(c - 1, 0)
        store(c - 1, (0,))
        add_bias(c - 1, 1)
        store(c - 1, (1,))
        h_quantize(c, (0, 1))
        last_matmul(c, 0, ps_s)
        last_matmul(c, 1, ps_z)
        add_bias(c - 1, 2)
        store(c - 1, (2,))
        h_empty(c, 1, "s", (0,))
        h_empty(c, 1, "v", (1,))
        add_bias(c - 1, 3)
        store(c - 1, (3,))
        add_bias(c, 0)
        store(c, (0,))
        h_quantize(c, (2, 3))
        last_matmul(c, 2)
        last_matmul(c, 3)
        add_bias(c, 1)
        store(c, (1,))
        add_bias(c, 2)
        store(c, (2,))
        add_bias(c, 3)
        store(c, (3,))
